import numpy as np
import ml_dtypes


def mxq(x, axis, fmt="e4m3"):
    dtype, down = {"e4m3": (ml_dtypes.float8_e4m3fn, 7), "e5m2": (ml_dtypes.float8_e5m2, 14)}[fmt]
    v = np.moveaxis(np.asarray(x, np.float32).astype(ml_dtypes.bfloat16).astype(np.float64), axis, -1)
    blocks = v.reshape(v.shape[:-1] + (-1, 32))
    amax = np.abs(blocks).max(-1, keepdims=True)
    byte = np.maximum(np.where(amax > 0, np.frexp(amax)[1] - 1 + 127, 0) - down, 1)
    scale = np.exp2(byte - 127.0)
    codes = (blocks / scale).astype(np.float32).astype(dtype).astype(np.float64)
    return np.moveaxis((codes * scale).reshape(v.shape), -1, axis)


WIDE = False


def mx_kscale(k):
    if not WIDE:
        return np.ones(k)
    levels = np.array([10, -10, 5, -5, 0])
    a = np.random.permutation(np.resize(levels, k // 512 * 4)).reshape(k // 512, 4)
    idx = np.arange(k)
    return np.exp2(a[idx // 512, idx % 128 // 32])


BF16 = ml_dtypes.bfloat16


def bf(x):
    return np.asarray(x, np.float32).astype(BF16)


def f64(x):
    return np.asarray(x).astype(np.float64)


B, N, C, F = 8, 32, 1024, 256
EPS_STD = 1e-5


def setup_inputs():
    u, s = mx_kscale(C), mx_kscale(C)
    rows = np.concatenate([u, u, s])
    return {"x": bf(np.random.standard_normal((B, N, C)) * u),
            "e_enc": bf(np.random.standard_normal((B, N, N, C)) * s),
            "W_pre": bf(np.random.standard_normal((3 * C, F)) / np.sqrt(3 * C) / rows[:, None]),
            "b_pre": bf(np.random.standard_normal(F) * 0.3)}


def reference(x, e_enc, W_pre, b_pre):
    w = f64(W_pre)
    xq = mxq(f64(x), 2, "e4m3")
    tgt = xq @ mxq(w[:C], 0, "e4m3")
    src = xq @ mxq(w[C:2 * C], 0, "e4m3")
    edg = mxq(f64(e_enc), 3, "e4m3") @ mxq(w[2 * C:], 0, "e4m3")
    m = tgt[:, :, None, :] + src[:, None, :, :] + edg + f64(b_pre)
    mean = m.mean(axis=2)
    mn = m.min(axis=2)
    mx = m.max(axis=2)
    var = (m * m).mean(axis=2) - mean * mean
    std = np.sqrt(np.maximum(var, 0.0) + EPS_STD)
    return np.concatenate([mean, mn, mx, std], axis=-1)

@@ -1,0 +1,305 @@
+from contextlib import ExitStack
+
+import concourse.mybir as mybir
+from concourse.masks import make_identity
+
+F32 = mybir.dt.float32
+BF16 = mybir.dt.bfloat16
+I32 = mybir.dt.int32
+U32 = mybir.dt.uint32
+U8 = mybir.dt.uint8
+FP8X4 = mybir.dt.float8_e4m3fn_x4
+ALU = mybir.AluOpType
+ACT = mybir.ActivationFunctionType
+AX = mybir.AxisListType
+
+P = 128
+B = 8
+N = 32
+C = 1024
+F = 256
+EPS_STD = 1e-5
+ROWS = 512
+NCH = B * N * N // ROWS
+TGT = ROWS // N
+FLOPS = 2 * C * F * (B * N * N + 2 * B * N)
+MANUAL = False
+LOOKAHEAD = 5
+
+
+def tile_gnnlayer_pa_t_kernel(tc, x, e_enc, W_pre, b_pre, out):
+    nc = tc.nc
+    with ExitStack() as ctx:
+        const = ctx.enter_context(tc.tile_pool(name="const", bufs=1))
+        epool = ctx.enter_context(tc.tile_pool(name="epool", bufs=6))
+        gpool = ctx.enter_context(tc.tile_pool(name="gpool", bufs=3))
+        qpool = ctx.enter_context(tc.tile_pool(name="qpool", bufs=3))
+        spool = ctx.enter_context(tc.tile_pool(name="spool", bufs=3))
+        tree = ctx.enter_context(tc.tile_pool(name="tree", bufs=2))
+        fpool = ctx.enter_context(tc.tile_pool(name="fpool", bufs=2))
+        tpsum = ctx.enter_context(tc.psum_pool(name="tpsum", bufs=4))
+        apsum = ctx.enter_context(tc.psum_pool(name="apsum", bufs=4))
+        if MANUAL:
+            ctx.enter_context(tc.manual_schedule())
+
+        one = const.tile([P, 1], F32, name="one")
+        nc.vector.memset(one[:], 1.0)
+        nc.scalar.sqrt(one[:], one[:])
+        ident = const.tile([P, P], F32, name="ident")
+        make_identity(nc, ident[:])
+
+        w_raw = const.tile([P, 12, 2, F], BF16, name="w_raw")
+        w_grp = const.tile([P, 6, F, 4], BF16, name="w_grp", align_bytes=64)
+        w_q = const.tile([P, 6, F], U32, name="w_q", align_bytes=64)
+        w_s = const.tile([P, 6, F], U8, name="w_s", align_bytes=64)
+        x_raw = const.tile([P, 2, C], BF16, name="x_raw")
+        x_grp = const.tile([P, 2, 2 * P, 2], F32, name="x_grp", align_bytes=64)
+        x_q = const.tile([P, 2, 2 * P], U32, name="x_q", align_bytes=64)
+        x_s = const.tile([P, 2, 2 * P], U8, name="x_s", align_bytes=64)
+        xr_q = const.tile([P, 2, B, P], U32, name="xr_q", align_bytes=64)
+        xr_s = const.tile([P, 2, B, P], U8, name="xr_s", align_bytes=64)
+        bias_bc = const.tile([P, F], BF16, name="bias_bc")
+        c_sb = const.tile([P, 2, F], F32, name="c_sb")
+        sums = const.tile([P, 2, B * N], F32, name="sums")
+        mins = const.tile([P, 2, B * N], F32, name="mins")
+        maxs = const.tile([P, 2, B * N], F32, name="maxs")
+        ssqs = const.tile([P, 2, B * N], F32, name="ssqs")
+
+        w_view = W_pre.rearrange("(s q e) c -> q s e c", q=P, e=2)
+        w_rows = w_raw[:].rearrange("p (s u) e c -> p s (u e) c", u=2)
+        e_view = e_enc.flatten_outer_dims().rearrange("(c t p) k -> c p t k", t=4, p=P)
+        out_rows = out.flatten_outer_dims()
+
+        ets = {}
+        grps = {}
+        codes = {}
+        accs = {}
+        sqs = {}
+
+        def load(c):
+            et = epool.tile([P, 4, C], BF16, name="et", tag="et")
+            nc.sync.dma_start(out=et[:], in_=e_view[c])
+            ets[c] = et
+
+        def transpose_rows(rows):
+            tp = tpsum.tile([P, 4, P], F32, name="tp", tag="tp")
+            words = rows.bitcast(F32)
+            for a in range(4):
+                nc.tensor.transpose(tp[:, a, :], words[:, a * P : (a + 1) * P], ident[:])
+            return tp
+
+        def evacuate(tp, dst):
+            nc.scalar.copy(out=dst, in_=tp[:].rearrange("p (g u) r -> p g r u", u=2))
+
+        def quantise(src, width, q_ap, s_ap):
+            nc.vector.quantize_mx(out=q_ap.bitcast(FP8X4), scales=s_ap, in_=src)
+
+        def regroup_w(eng_copy, s):
+            eng_copy(
+                out=w_grp[:, s].rearrange("p (c i) t -> p c t i", i=4),
+                in_=w_rows[:, s].rearrange("p t (c i) -> p c t i", i=4),
+            )
+
+        nc.sync.dma_start(out=w_raw[:, 4:12], in_=w_view[:, 4:12])
+        nc.sync.dma_start(out=x_raw[:], in_=x.flatten_outer_dims().rearrange("(t p) k -> p t k", p=P))
+        load(0)
+        load(1)
+        load(2)
+        nc.sync.dma_start(out=w_raw[:, 0:4], in_=w_view[:, 0:4])
+        nc.sync.dma_start(out=bias_bc[:], in_=b_pre.partition_broadcast(P))
+        load(3)
+        load(4)
+
+        for s in range(2, 6):
+            regroup_w(nc.vector.tensor_copy, s)
+        quantise(
+            w_grp[:, 2:6].rearrange("p s c t -> p (s c t)"),
+            4096,
+            w_q[:, 2:6].rearrange("p s c -> p (s c)"),
+            w_s[:, 2:6].rearrange("p s c -> p (s c)"),
+        )
+
+        nc.vector.memset(x_s[:].rearrange("p g n -> p (g n)").bitcast(I32), 0)
+        for t in range(2):
+            tp = transpose_rows(x_raw[:, t, :])
+            evacuate(tp, x_grp[:, :, t * P : (t + 1) * P, :])
+        quantise(
+            x_grp[:].rearrange("p g n u -> p (g n u)").bitcast(BF16),
+            2048,
+            x_q[:].rearrange("p g n -> p (g n)"),
+            x_s[:].rearrange("p g n -> p (g n)"),
+        )
+        nc.vector.tensor_copy(
+            out=xr_q[:].bitcast(I32).rearrange("p g b (d j) -> p (g b) d j", d=4),
+            in_=x_q[:].bitcast(I32).rearrange("p g (b j) -> p (g b) j", j=N).unsqueeze(2).to_broadcast([P, 2 * B, 4, N]),
+        )
+        nc.vector.tensor_copy(
+            out=xr_s[:].bitcast(I32).rearrange("p g b (d j) -> p (g b) d j", d=4),
+            in_=x_s[:].bitcast(I32).rearrange("p g (b j) -> p (g b) j", j=N // 4).unsqueeze(2).to_broadcast([P, 2 * B, 4, N // 4]),
+        )
+
+        def front(c):
+            grp = gpool.tile([P, 2, ROWS, 2], F32, name="grp", tag="grp", align_bytes=64)
+            for t in range(4):
+                tp = transpose_rows(ets[c][:, t, :])
+                evacuate(tp, grp[:, :, t * P : (t + 1) * P, :])
+            grps[c] = grp
+
+        def quantise_chunk(c):
+            eq = qpool.tile([P, 2, ROWS], U32, name="eq", tag="eq", align_bytes=64)
+            es = qpool.tile([P, 2, ROWS], U8, name="es", tag="es", align_bytes=64)
+            quantise(
+                grps[c][:].rearrange("p g n u -> p (g n u)").bitcast(BF16),
+                4096,
+                eq[:].rearrange("p g n -> p (g n)"),
+                es[:].rearrange("p g n -> p (g n)"),
+            )
+            codes[c] = (eq, es)
+
+        def mx(out_ap, s, cols, rhs, rhs_scale, start, stop):
+            nc.tensor.matmul_mx(
+                out=out_ap,
+                lhsT=w_q[:, s, cols].bitcast(FP8X4),
+                lhsT_scale=w_s[:, s, cols],
+                rhs=rhs.bitcast(FP8X4),
+                rhs_scale=rhs_scale,
+                start=start,
+                stop=stop,
+            )
+
+        def messages(c):
+            b = c // 2
+            eq, es = codes[c]
+            sq = spool.tile([P, 2, ROWS], F32, name="sq", tag="sq")
+            pair = []
+            for ft in range(2):
+                cols = slice(ft * P, (ft + 1) * P)
+                acc = apsum.tile([P, ROWS], F32, name="acc", tag="acc")
+                mx(acc[:], 4, cols, eq[:, 0, :], es[:, 0, :], True, False)
+                for g in range(2):
+                    for q in range(4):
+                        mx(acc[:, q * P : (q + 1) * P], 2 + g, cols, xr_q[:, g, b, :], xr_s[:, g, b, :], False, False)
+                mx(acc[:], 5, cols, eq[:, 1, :], es[:, 1, :], False, True)
+                nc.scalar.activation(out=sq[:, ft, :], in_=acc[:], func=ACT.Square)
+                pair.append(acc)
+            accs[c] = pair
+            sqs[c] = sq
+
+        def reduces(c):
+            cols = slice(c * TGT, (c + 1) * TGT)
+            for ft in range(2):
+                m = accs[c][ft][:].rearrange("p (i j) -> p i j", j=N)
+                nc.vector.tensor_reduce(out=maxs[:, ft, cols], in_=m, axis=AX.X, op=ALU.max)
+                nc.vector.tensor_reduce(out=mins[:, ft, cols], in_=m, axis=AX.X, op=ALU.min)
+                nc.vector.tensor_reduce(out=sums[:, ft, cols], in_=m, axis=AX.X, op=ALU.add)
+
+        def square_sums(c):
+            cols = slice(c * TGT, (c + 1) * TGT)
+            cur = sqs[c][:].rearrange("p f (i j) -> p (f i) j", j=N)
+            for width in (16, 8, 4, 2):
+                nxt = tree.tile([P, 2 * TGT, width], F32, name="lvl%d" % width, tag="lvl%d" % width)
+                nc.gpsimd.tensor_tensor(out=nxt[:], in0=cur[:, :, 0:width], in1=cur[:, :, width : 2 * width], op=ALU.add)
+                cur = nxt[:]
+            last = cur.rearrange("p (f i) j -> p f i j", f=2)
+            nc.gpsimd.tensor_tensor(out=ssqs[:, :, cols], in0=last[:, :, :, 0], in1=last[:, :, :, 1], op=ALU.add)
+
+        def target_weights():
+            for s in range(2):
+                regroup_w(nc.scalar.copy, s)
+
+        def target_term():
+            quantise(
+                w_grp[:, 0:2].rearrange("p s c t -> p (s c t)"),
+                2048,
+                w_q[:, 0:2].rearrange("p s c -> p (s c)"),
+                w_s[:, 0:2].rearrange("p s c -> p (s c)"),
+            )
+            tg = apsum.tile([P, 2, F], F32, name="tg", tag="acc")
+            for hb in range(2):
+                for g in range(2):
+                    nc.tensor.matmul_mx(
+                        out=tg[:, hb, :],
+                        lhsT=x_q[:, g, hb * P : (hb + 1) * P].bitcast(FP8X4),
+                        lhsT_scale=x_s[:, g, hb * P : (hb + 1) * P],
+                        rhs=w_q[:, g, :].bitcast(FP8X4),
+                        rhs_scale=w_s[:, g, :],
+                        start=(g == 0),
+                        stop=(g == 1),
+                    )
+            nc.vector.tensor_tensor(
+                out=c_sb[:], in0=tg[:], in1=bias_bc[:].unsqueeze(1).to_broadcast([P, 2, F]), op=ALU.add
+            )
+
+        fin = {}
+
+        def finish_math(hb):
+            cols = slice(hb * P, (hb + 1) * P)
+            mean = fpool.tile([P, 2, P], F32, name="mean", tag="mean")
+            msq = fpool.tile([P, 2, P], F32, name="msq", tag="msq")
+            var = fpool.tile([P, 2, P], F32, name="var", tag="var")
+            std = fpool.tile([P, 2, P], F32, name="std", tag="std")
+            nc.vector.tensor_scalar_mul(out=mean[:], in0=sums[:, :, cols], scalar1=1.0 / N)
+            nc.vector.tensor_tensor(out=msq[:], in0=mean[:], in1=mean[:], op=ALU.mult)
+            nc.vector.scalar_tensor_tensor(
+                out=var[:], in0=ssqs[:, :, cols], scalar=1.0 / N, in1=msq[:], op0=ALU.mult, op1=ALU.subtract
+            )
+            nc.vector.tensor_scalar(out=var[:], in0=var[:], scalar1=0.0, scalar2=EPS_STD, op0=ALU.max, op1=ALU.add)
+            nc.scalar.sqrt(std[:], var[:])
+            fin[hb] = (mean, std)
+
+        def finish_transposes(hb):
+            cols = slice(hb * P, (hb + 1) * P)
+            mean, std = fin[hb]
+            f0 = tpsum.tile([P, 4, P], F32, name="f0", tag="tp")
+            f1 = tpsum.tile([P, 4, P], F32, name="f1", tag="tp")
+            for ft in range(2):
+                nc.tensor.transpose(f0[:, ft, :], mean[:, ft, :], ident[:])
+            for ft in range(2):
+                nc.tensor.transpose(f0[:, 2 + ft, :], mins[:, ft, cols], ident[:])
+            for ft in range(2):
+                nc.tensor.transpose(f1[:, ft, :], maxs[:, ft, cols], ident[:])
+            for ft in range(2):
+                nc.tensor.transpose(f1[:, 2 + ft, :], std[:, ft, :], ident[:])
+            fin[hb] = (f0, f1)
+
+        def finish_store(hb):
+            f0, f1 = fin[hb]
+            osb = fpool.tile([P, 4, F], F32, name="osb", tag="osb")
+            shift = c_sb[:, hb, :]
+            nc.vector.tensor_tensor(
+                out=osb[:, 0:2, :],
+                in0=f0[:].rearrange("p (s f) r -> p s (f r)", f=2),
+                in1=shift.unsqueeze(1).to_broadcast([P, 2, F]),
+                op=ALU.add,
+            )
+            nc.vector.tensor_tensor(
+                out=osb[:, 2, :], in0=f1[:, 0:2, :].rearrange("p f r -> p (f r)"), in1=shift, op=ALU.add
+            )
+            nc.scalar.copy(out=osb[:, 3, :], in_=f1[:, 2:4, :].rearrange("p f r -> p (f r)"))
+            nc.sync.dma_start(out=out_rows[hb * P : (hb + 1) * P, :], in_=osb[:].rearrange("p s f -> p (s f)"))
+
+        for n in range(-2, NCH + 1):
+            if n >= 0 and n + LOOKAHEAD < NCH:
+                load(n + LOOKAHEAD)
+            if n == 11:
+                finish_transposes(0)
+            if 0 <= n + 2 < NCH:
+                front(n + 2)
+            if n == 3:
+                target_weights()
+            if n == 5:
+                target_term()
+            if 0 <= n < NCH:
+                messages(n)
+            if n == 10:
+                finish_math(0)
+            if n == 12:
+                finish_store(0)
+            if 0 <= n + 1 < NCH:
+                quantise_chunk(n + 1)
+            if 0 <= n - 1 < NCH:
+                reduces(n - 1)
+                square_sums(n - 1)
+        finish_math(1)
+        finish_transposes(1)
+        finish_store(1)

@@ -23,7 +23,7 @@ ROWS = 512
 NCH = B * N * N // ROWS
 TGT = ROWS // N
 FLOPS = 2 * C * F * (B * N * N + 2 * B * N)
-MANUAL = False
+MANUAL = True
 LOOKAHEAD = 5
 
 
@@ -76,9 +76,11 @@ def tile_gnnlayer_pa_t_kernel(tc, x, e_enc, W_pre, b_pre, out):
         accs = {}
         sqs = {}
 
-        def load(c):
+        def load(c, pieces=1):
             et = epool.tile([P, 4, C], BF16, name="et", tag="et")
-            nc.sync.dma_start(out=et[:], in_=e_view[c])
+            step = 4 // pieces
+            for t in range(0, 4, step):
+                nc.sync.dma_start(out=et[:, t : t + step, :], in_=e_view[c][:, t : t + step, :])
             ets[c] = et
 
         def transpose_rows(rows):
@@ -102,7 +104,7 @@ def tile_gnnlayer_pa_t_kernel(tc, x, e_enc, W_pre, b_pre, out):
 
         nc.sync.dma_start(out=w_raw[:, 4:12], in_=w_view[:, 4:12])
         nc.sync.dma_start(out=x_raw[:], in_=x.flatten_outer_dims().rearrange("(t p) k -> p t k", p=P))
-        load(0)
+        load(0, 4)
         load(1)
         load(2)
         nc.sync.dma_start(out=w_raw[:, 0:4], in_=w_view[:, 0:4])
@@ -207,13 +209,15 @@ def tile_gnnlayer_pa_t_kernel(tc, x, e_enc, W_pre, b_pre, out):
             for s in range(2):
                 regroup_w(nc.scalar.copy, s)
 
-        def target_term():
+        def target_quantise():
             quantise(
                 w_grp[:, 0:2].rearrange("p s c t -> p (s c t)"),
                 2048,
                 w_q[:, 0:2].rearrange("p s c -> p (s c)"),
                 w_s[:, 0:2].rearrange("p s c -> p (s c)"),
             )
+
+        def target_term():
             tg = apsum.tile([P, 2, F], F32, name="tg", tag="acc")
             for hb in range(2):
                 for g in range(2):
@@ -281,20 +285,22 @@ def tile_gnnlayer_pa_t_kernel(tc, x, e_enc, W_pre, b_pre, out):
         for n in range(-2, NCH + 1):
             if n >= 0 and n + LOOKAHEAD < NCH:
                 load(n + LOOKAHEAD)
-            if n == 11:
-                finish_transposes(0)
             if 0 <= n + 2 < NCH:
                 front(n + 2)
-            if n == 3:
+            if n == 11:
+                finish_transposes(0)
+            if n == 2:
                 target_weights()
-            if n == 5:
+            if n == 4:
                 target_term()
             if 0 <= n < NCH:
                 messages(n)
-            if n == 10:
+            if n == 9:
                 finish_math(0)
-            if n == 12:
+            if n == 11:
                 finish_store(0)
+            if n == 3:
+                target_quantise()
             if 0 <= n + 1 < NCH:
                 quantise_chunk(n + 1)
             if 0 <= n - 1 < NCH:

@@ -23,7 +23,7 @@ ROWS = 512
 NCH = B * N * N // ROWS
 TGT = ROWS // N
 FLOPS = 2 * C * F * (B * N * N + 2 * B * N)
-MANUAL = True
+MANUAL = False
 LOOKAHEAD = 5
 
 
@@ -34,8 +34,6 @@ def tile_gnnlayer_pa_t_kernel(tc, x, e_enc, W_pre, b_pre, out):
         epool = ctx.enter_context(tc.tile_pool(name="epool", bufs=6))
         gpool = ctx.enter_context(tc.tile_pool(name="gpool", bufs=3))
         qpool = ctx.enter_context(tc.tile_pool(name="qpool", bufs=3))
-        spool = ctx.enter_context(tc.tile_pool(name="spool", bufs=3))
-        tree = ctx.enter_context(tc.tile_pool(name="tree", bufs=2))
         fpool = ctx.enter_context(tc.tile_pool(name="fpool", bufs=2))
         tpsum = ctx.enter_context(tc.psum_pool(name="tpsum", bufs=4))
         apsum = ctx.enter_context(tc.psum_pool(name="apsum", bufs=4))
@@ -60,10 +58,11 @@ def tile_gnnlayer_pa_t_kernel(tc, x, e_enc, W_pre, b_pre, out):
         xr_s = const.tile([P, 2, B, P], U8, name="xr_s", align_bytes=64)
         bias_bc = const.tile([P, F], BF16, name="bias_bc")
         c_sb = const.tile([P, 2, F], F32, name="c_sb")
-        sums = const.tile([P, 2, B * N], F32, name="sums")
+        bst = const.tile([P, 2, B * N, 3], F32, name="bst")
+        eps_t = const.tile([P, 1], F32, name="eps_t")
+        nc.vector.memset(eps_t[:], EPS_STD)
         mins = const.tile([P, 2, B * N], F32, name="mins")
         maxs = const.tile([P, 2, B * N], F32, name="maxs")
-        ssqs = const.tile([P, 2, B * N], F32, name="ssqs")
 
         w_view = W_pre.rearrange("(s q e) c -> q s e c", q=P, e=2)
         w_rows = w_raw[:].rearrange("p (s u) e c -> p s (u e) c", u=2)
@@ -74,7 +73,6 @@ def tile_gnnlayer_pa_t_kernel(tc, x, e_enc, W_pre, b_pre, out):
         grps = {}
         codes = {}
         accs = {}
-        sqs = {}
 
         def load(c, pieces=1):
             et = epool.tile([P, 4, C], BF16, name="et", tag="et")
@@ -172,7 +170,6 @@ def tile_gnnlayer_pa_t_kernel(tc, x, e_enc, W_pre, b_pre, out):
         def messages(c):
             b = c // 2
             eq, es = codes[c]
-            sq = spool.tile([P, 2, ROWS], F32, name="sq", tag="sq")
             pair = []
             for ft in range(2):
                 cols = slice(ft * P, (ft + 1) * P)
@@ -182,10 +179,8 @@ def tile_gnnlayer_pa_t_kernel(tc, x, e_enc, W_pre, b_pre, out):
                     for q in range(4):
                         mx(acc[:, q * P : (q + 1) * P], 2 + g, cols, xr_q[:, g, b, :], xr_s[:, g, b, :], False, False)
                 mx(acc[:], 5, cols, eq[:, 1, :], es[:, 1, :], False, True)
-                nc.scalar.activation(out=sq[:, ft, :], in_=acc[:], func=ACT.Square)
                 pair.append(acc)
             accs[c] = pair
-            sqs[c] = sq
 
         def reduces(c):
             cols = slice(c * TGT, (c + 1) * TGT)
@@ -193,31 +188,23 @@ def tile_gnnlayer_pa_t_kernel(tc, x, e_enc, W_pre, b_pre, out):
                 m = accs[c][ft][:].rearrange("p (i j) -> p i j", j=N)
                 nc.vector.tensor_reduce(out=maxs[:, ft, cols], in_=m, axis=AX.X, op=ALU.max)
                 nc.vector.tensor_reduce(out=mins[:, ft, cols], in_=m, axis=AX.X, op=ALU.min)
-                nc.vector.tensor_reduce(out=sums[:, ft, cols], in_=m, axis=AX.X, op=ALU.add)
-
-        def square_sums(c):
-            cols = slice(c * TGT, (c + 1) * TGT)
-            cur = sqs[c][:].rearrange("p f (i j) -> p (f i) j", j=N)
-            for width in (16, 8, 4, 2):
-                nxt = tree.tile([P, 2 * TGT, width], F32, name="lvl%d" % width, tag="lvl%d" % width)
-                nc.gpsimd.tensor_tensor(out=nxt[:], in0=cur[:, :, 0:width], in1=cur[:, :, width : 2 * width], op=ALU.add)
-                cur = nxt[:]
-            last = cur.rearrange("p (f i) j -> p f i j", f=2)
-            nc.gpsimd.tensor_tensor(out=ssqs[:, :, cols], in0=last[:, :, :, 0], in1=last[:, :, :, 1], op=ALU.add)
+                for i in range(0, TGT, 2):
+                    nc.vector.bn_stats(
+                        out=bst[:, ft, c * TGT + i : c * TGT + i + 2, :].rearrange("p m s -> p (m s)"),
+                        in_=m[:, i : i + 2, :].rearrange("p m j -> p j m"),
+                    )
 
         def target_weights():
             for s in range(2):
                 regroup_w(nc.scalar.copy, s)
 
-        def target_quantise():
+        def target_term():
             quantise(
                 w_grp[:, 0:2].rearrange("p s c t -> p (s c t)"),
                 2048,
                 w_q[:, 0:2].rearrange("p s c -> p (s c)"),
                 w_s[:, 0:2].rearrange("p s c -> p (s c)"),
             )
-
-        def target_term():
             tg = apsum.tile([P, 2, F], F32, name="tg", tag="acc")
             for hb in range(2):
                 for g in range(2):
@@ -239,16 +226,11 @@ def tile_gnnlayer_pa_t_kernel(tc, x, e_enc, W_pre, b_pre, out):
         def finish_math(hb):
             cols = slice(hb * P, (hb + 1) * P)
             mean = fpool.tile([P, 2, P], F32, name="mean", tag="mean")
-            msq = fpool.tile([P, 2, P], F32, name="msq", tag="msq")
             var = fpool.tile([P, 2, P], F32, name="var", tag="var")
             std = fpool.tile([P, 2, P], F32, name="std", tag="std")
-            nc.vector.tensor_scalar_mul(out=mean[:], in0=sums[:, :, cols], scalar1=1.0 / N)
-            nc.vector.tensor_tensor(out=msq[:], in0=mean[:], in1=mean[:], op=ALU.mult)
-            nc.vector.scalar_tensor_tensor(
-                out=var[:], in0=ssqs[:, :, cols], scalar=1.0 / N, in1=msq[:], op0=ALU.mult, op1=ALU.subtract
-            )
-            nc.vector.tensor_scalar(out=var[:], in0=var[:], scalar1=0.0, scalar2=EPS_STD, op0=ALU.max, op1=ALU.add)
-            nc.scalar.sqrt(std[:], var[:])
+            nc.scalar.copy(out=mean[:], in_=bst[:, :, cols, 1])
+            nc.vector.tensor_scalar(out=var[:], in0=bst[:, :, cols, 2], scalar1=1.0 / N, scalar2=0.0, op0=ALU.mult, op1=ALU.max)
+            nc.scalar.activation(out=std[:], in_=var[:], func=ACT.Sqrt, bias=eps_t[:])
             fin[hb] = (mean, std)
 
         def finish_transposes(hb):
@@ -285,27 +267,24 @@ def tile_gnnlayer_pa_t_kernel(tc, x, e_enc, W_pre, b_pre, out):
         for n in range(-2, NCH + 1):
             if n >= 0 and n + LOOKAHEAD < NCH:
                 load(n + LOOKAHEAD)
-            if 0 <= n + 2 < NCH:
-                front(n + 2)
             if n == 11:
                 finish_transposes(0)
-            if n == 2:
+            if 0 <= n + 2 < NCH:
+                front(n + 2)
+            if n == 3:
                 target_weights()
-            if n == 4:
+            if n == 5:
                 target_term()
             if 0 <= n < NCH:
                 messages(n)
-            if n == 9:
+            if n == 10:
                 finish_math(0)
-            if n == 11:
+            if n == 12:
                 finish_store(0)
-            if n == 3:
-                target_quantise()
             if 0 <= n + 1 < NCH:
                 quantise_chunk(n + 1)
             if 0 <= n - 1 < NCH:
                 reduces(n - 1)
-                square_sums(n - 1)
         finish_math(1)
         finish_transposes(1)
         finish_store(1)

@@ -34,6 +34,8 @@ def tile_gnnlayer_pa_t_kernel(tc, x, e_enc, W_pre, b_pre, out):
         epool = ctx.enter_context(tc.tile_pool(name="epool", bufs=6))
         gpool = ctx.enter_context(tc.tile_pool(name="gpool", bufs=3))
         qpool = ctx.enter_context(tc.tile_pool(name="qpool", bufs=3))
+        spool = ctx.enter_context(tc.tile_pool(name="spool", bufs=3))
+        tree = ctx.enter_context(tc.tile_pool(name="tree", bufs=2))
         fpool = ctx.enter_context(tc.tile_pool(name="fpool", bufs=2))
         tpsum = ctx.enter_context(tc.psum_pool(name="tpsum", bufs=4))
         apsum = ctx.enter_context(tc.psum_pool(name="apsum", bufs=4))
@@ -58,7 +60,8 @@ def tile_gnnlayer_pa_t_kernel(tc, x, e_enc, W_pre, b_pre, out):
         xr_s = const.tile([P, 2, B, P], U8, name="xr_s", align_bytes=64)
         bias_bc = const.tile([P, F], BF16, name="bias_bc")
         c_sb = const.tile([P, 2, F], F32, name="c_sb")
-        bst = const.tile([P, 2, B * N, 3], F32, name="bst")
+        bst = const.tile([P, B * N, 3], F32, name="bst")
+        s12 = const.tile([P, 2, B * N], F32, name="s12")
         eps_t = const.tile([P, 1], F32, name="eps_t")
         nc.vector.memset(eps_t[:], EPS_STD)
         mins = const.tile([P, 2, B * N], F32, name="mins")
@@ -73,6 +76,7 @@ def tile_gnnlayer_pa_t_kernel(tc, x, e_enc, W_pre, b_pre, out):
         grps = {}
         codes = {}
         accs = {}
+        planes = {}
 
         def load(c, pieces=1):
             et = epool.tile([P, 4, C], BF16, name="et", tag="et")
@@ -180,7 +184,11 @@ def tile_gnnlayer_pa_t_kernel(tc, x, e_enc, W_pre, b_pre, out):
                         mx(acc[:, q * P : (q + 1) * P], 2 + g, cols, xr_q[:, g, b, :], xr_s[:, g, b, :], False, False)
                 mx(acc[:], 5, cols, eq[:, 1, :], es[:, 1, :], False, True)
                 pair.append(acc)
+            pl = spool.tile([P, 2, ROWS], F32, name="pl", tag="pl")
+            nc.scalar.copy(out=pl[:, 0, :], in_=pair[1][:])
+            nc.scalar.activation(out=pl[:, 1, :], in_=pair[1][:], func=ACT.Square)
             accs[c] = pair
+            planes[c] = pl
 
         def reduces(c):
             cols = slice(c * TGT, (c + 1) * TGT)
@@ -188,11 +196,22 @@ def tile_gnnlayer_pa_t_kernel(tc, x, e_enc, W_pre, b_pre, out):
                 m = accs[c][ft][:].rearrange("p (i j) -> p i j", j=N)
                 nc.vector.tensor_reduce(out=maxs[:, ft, cols], in_=m, axis=AX.X, op=ALU.max)
                 nc.vector.tensor_reduce(out=mins[:, ft, cols], in_=m, axis=AX.X, op=ALU.min)
-                for i in range(0, TGT, 2):
-                    nc.vector.bn_stats(
-                        out=bst[:, ft, c * TGT + i : c * TGT + i + 2, :].rearrange("p m s -> p (m s)"),
-                        in_=m[:, i : i + 2, :].rearrange("p m j -> p j m"),
-                    )
+                if ft == 0:
+                    for i in range(0, TGT, 2):
+                        nc.vector.bn_stats(
+                            out=bst[:, c * TGT + i : c * TGT + i + 2, :].rearrange("p m s -> p (m s)"),
+                            in_=m[:, i : i + 2, :].rearrange("p m j -> p j m"),
+                        )
+
+        def plane_sums(c):
+            cols = slice(c * TGT, (c + 1) * TGT)
+            cur = planes[c][:].rearrange("p f (i j) -> p (f i) j", j=N)
+            for width in (16, 8, 4, 2):
+                nxt = tree.tile([P, 2 * TGT, width], F32, name="lvl%d" % width, tag="lvl%d" % width)
+                nc.gpsimd.tensor_tensor(out=nxt[:], in0=cur[:, :, 0:width], in1=cur[:, :, width : 2 * width], op=ALU.add)
+                cur = nxt[:]
+            last = cur.rearrange("p (f i) j -> p f i j", f=2)
+            nc.gpsimd.tensor_tensor(out=s12[:, :, cols], in0=last[:, :, :, 0], in1=last[:, :, :, 1], op=ALU.add)
 
         def target_weights():
             for s in range(2):
@@ -228,8 +247,15 @@ def tile_gnnlayer_pa_t_kernel(tc, x, e_enc, W_pre, b_pre, out):
             mean = fpool.tile([P, 2, P], F32, name="mean", tag="mean")
             var = fpool.tile([P, 2, P], F32, name="var", tag="var")
             std = fpool.tile([P, 2, P], F32, name="std", tag="std")
-            nc.scalar.copy(out=mean[:], in_=bst[:, :, cols, 1])
-            nc.vector.tensor_scalar(out=var[:], in0=bst[:, :, cols, 2], scalar1=1.0 / N, scalar2=0.0, op0=ALU.mult, op1=ALU.max)
+            msq = fpool.tile([P, P], F32, name="msq", tag="msq")
+            nc.scalar.copy(out=mean[:, 0, :], in_=bst[:, cols, 1])
+            nc.scalar.mul(out=mean[:, 1, :], in_=s12[:, 0, cols], mul=1.0 / N)
+            nc.scalar.activation(out=msq[:], in_=s12[:, 0, cols], func=ACT.Square, scale=1.0 / N)
+            nc.vector.tensor_scalar_mul(out=var[:, 0, :], in0=bst[:, cols, 2], scalar1=1.0 / N)
+            nc.vector.scalar_tensor_tensor(
+                out=var[:, 1, :], in0=s12[:, 1, cols], scalar=1.0 / N, in1=msq[:], op0=ALU.mult, op1=ALU.subtract
+            )
+            nc.vector.tensor_scalar_max(out=var[:], in0=var[:], scalar1=0.0)
             nc.scalar.activation(out=std[:], in_=var[:], func=ACT.Sqrt, bias=eps_t[:])
             fin[hb] = (mean, std)
 
@@ -285,6 +311,7 @@ def tile_gnnlayer_pa_t_kernel(tc, x, e_enc, W_pre, b_pre, out):
                 quantise_chunk(n + 1)
             if 0 <= n - 1 < NCH:
                 reduces(n - 1)
+                plane_sums(n - 1)
         finish_math(1)
         finish_transposes(1)
         finish_store(1)

@@ -23,8 +23,7 @@ ROWS = 512
 NCH = B * N * N // ROWS
 TGT = ROWS // N
 FLOPS = 2 * C * F * (B * N * N + 2 * B * N)
-MANUAL = False
-LOOKAHEAD = 5
+PRELOAD = 5
 
 
 def tile_gnnlayer_pa_t_kernel(tc, x, e_enc, W_pre, b_pre, out):
@@ -39,15 +38,11 @@ def tile_gnnlayer_pa_t_kernel(tc, x, e_enc, W_pre, b_pre, out):
         fpool = ctx.enter_context(tc.tile_pool(name="fpool", bufs=2))
         tpsum = ctx.enter_context(tc.psum_pool(name="tpsum", bufs=4))
         apsum = ctx.enter_context(tc.psum_pool(name="apsum", bufs=4))
-        if MANUAL:
-            ctx.enter_context(tc.manual_schedule())
+        ctx.enter_context(tc.manual_schedule())
 
-        one = const.tile([P, 1], F32, name="one")
-        nc.vector.memset(one[:], 1.0)
-        nc.scalar.sqrt(one[:], one[:])
+        eps_t = const.tile([P, 1], F32, name="eps_t")
+        warm = const.tile([P, 1], F32, name="warm")
         ident = const.tile([P, P], F32, name="ident")
-        make_identity(nc, ident[:])
-
         w_raw = const.tile([P, 12, 2, F], BF16, name="w_raw")
         w_grp = const.tile([P, 6, F, 4], BF16, name="w_grp", align_bytes=64)
         w_q = const.tile([P, 6, F], U32, name="w_q", align_bytes=64)
@@ -59,11 +54,10 @@ def tile_gnnlayer_pa_t_kernel(tc, x, e_enc, W_pre, b_pre, out):
         xr_q = const.tile([P, 2, B, P], U32, name="xr_q", align_bytes=64)
         xr_s = const.tile([P, 2, B, P], U8, name="xr_s", align_bytes=64)
         bias_bc = const.tile([P, F], BF16, name="bias_bc")
+        c_raw = const.tile([P, 2, F], F32, name="c_raw")
         c_sb = const.tile([P, 2, F], F32, name="c_sb")
         bst = const.tile([P, B * N, 3], F32, name="bst")
         s12 = const.tile([P, 2, B * N], F32, name="s12")
-        eps_t = const.tile([P, 1], F32, name="eps_t")
-        nc.vector.memset(eps_t[:], EPS_STD)
         mins = const.tile([P, 2, B * N], F32, name="mins")
         maxs = const.tile([P, 2, B * N], F32, name="maxs")
 
@@ -77,6 +71,7 @@ def tile_gnnlayer_pa_t_kernel(tc, x, e_enc, W_pre, b_pre, out):
         codes = {}
         accs = {}
         planes = {}
+        fin = {}
 
         def load(c, pieces=1):
             et = epool.tile([P, 4, C], BF16, name="et", tag="et")
@@ -84,6 +79,9 @@ def tile_gnnlayer_pa_t_kernel(tc, x, e_enc, W_pre, b_pre, out):
             for t in range(0, 4, step):
                 nc.sync.dma_start(out=et[:, t : t + step, :], in_=e_view[c][:, t : t + step, :])
             ets[c] = et
+
+        def load_w(block):
+            nc.sync.dma_start(out=w_raw[:, 4 * block : 4 * block + 4], in_=w_view[:, 4 * block : 4 * block + 4])
 
         def transpose_rows(rows):
             tp = tpsum.tile([P, 4, P], F32, name="tp", tag="tp")
@@ -95,52 +93,32 @@ def tile_gnnlayer_pa_t_kernel(tc, x, e_enc, W_pre, b_pre, out):
         def evacuate(tp, dst):
             nc.scalar.copy(out=dst, in_=tp[:].rearrange("p (g u) r -> p g r u", u=2))
 
-        def quantise(src, width, q_ap, s_ap):
+        def quantise(src, q_ap, s_ap):
             nc.vector.quantize_mx(out=q_ap.bitcast(FP8X4), scales=s_ap, in_=src)
 
-        def regroup_w(eng_copy, s):
-            eng_copy(
-                out=w_grp[:, s].rearrange("p (c i) t -> p c t i", i=4),
-                in_=w_rows[:, s].rearrange("p t (c i) -> p c t i", i=4),
+        def quantise_w(block):
+            lo = 2 * block
+            quantise(
+                w_grp[:, lo : lo + 2].rearrange("p s c t -> p (s c t)"),
+                w_q[:, lo : lo + 2].rearrange("p s c -> p (s c)"),
+                w_s[:, lo : lo + 2].rearrange("p s c -> p (s c)"),
             )
 
-        nc.sync.dma_start(out=w_raw[:, 4:12], in_=w_view[:, 4:12])
-        nc.sync.dma_start(out=x_raw[:], in_=x.flatten_outer_dims().rearrange("(t p) k -> p t k", p=P))
-        load(0, 4)
-        load(1)
-        load(2)
-        nc.sync.dma_start(out=w_raw[:, 0:4], in_=w_view[:, 0:4])
-        nc.sync.dma_start(out=bias_bc[:], in_=b_pre.partition_broadcast(P))
-        load(3)
-        load(4)
+        def regroup_views(s):
+            return (
+                w_grp[:, s].rearrange("p (c i) t -> p c t i", i=4),
+                w_rows[:, s].rearrange("p t (c i) -> p c t i", i=4),
+            )
 
-        for s in range(2, 6):
-            regroup_w(nc.vector.tensor_copy, s)
-        quantise(
-            w_grp[:, 2:6].rearrange("p s c t -> p (s c t)"),
-            4096,
-            w_q[:, 2:6].rearrange("p s c -> p (s c)"),
-            w_s[:, 2:6].rearrange("p s c -> p (s c)"),
-        )
+        def regroup_w_vector(block):
+            for s in (2 * block, 2 * block + 1):
+                dst, src = regroup_views(s)
+                nc.vector.tensor_copy(out=dst, in_=src)
 
-        nc.vector.memset(x_s[:].rearrange("p g n -> p (g n)").bitcast(I32), 0)
-        for t in range(2):
-            tp = transpose_rows(x_raw[:, t, :])
-            evacuate(tp, x_grp[:, :, t * P : (t + 1) * P, :])
-        quantise(
-            x_grp[:].rearrange("p g n u -> p (g n u)").bitcast(BF16),
-            2048,
-            x_q[:].rearrange("p g n -> p (g n)"),
-            x_s[:].rearrange("p g n -> p (g n)"),
-        )
-        nc.vector.tensor_copy(
-            out=xr_q[:].bitcast(I32).rearrange("p g b (d j) -> p (g b) d j", d=4),
-            in_=x_q[:].bitcast(I32).rearrange("p g (b j) -> p (g b) j", j=N).unsqueeze(2).to_broadcast([P, 2 * B, 4, N]),
-        )
-        nc.vector.tensor_copy(
-            out=xr_s[:].bitcast(I32).rearrange("p g b (d j) -> p (g b) d j", d=4),
-            in_=x_s[:].bitcast(I32).rearrange("p g (b j) -> p (g b) j", j=N // 4).unsqueeze(2).to_broadcast([P, 2 * B, 4, N // 4]),
-        )
+        def regroup_w_gpsimd(block):
+            for s in (2 * block, 2 * block + 1):
+                dst, src = regroup_views(s)
+                nc.gpsimd.tensor_scalar(out=dst, in0=src, scalar1=1.0, scalar2=0.0, op0=ALU.mult, op1=ALU.add)
 
         def front(c):
             grp = gpool.tile([P, 2, ROWS, 2], F32, name="grp", tag="grp", align_bytes=64)
@@ -154,7 +132,6 @@ def tile_gnnlayer_pa_t_kernel(tc, x, e_enc, W_pre, b_pre, out):
             es = qpool.tile([P, 2, ROWS], U8, name="es", tag="es", align_bytes=64)
             quantise(
                 grps[c][:].rearrange("p g n u -> p (g n u)").bitcast(BF16),
-                4096,
                 eq[:].rearrange("p g n -> p (g n)"),
                 es[:].rearrange("p g n -> p (g n)"),
             )
@@ -174,8 +151,8 @@ def tile_gnnlayer_pa_t_kernel(tc, x, e_enc, W_pre, b_pre, out):
         def messages(c):
             b = c // 2
             eq, es = codes[c]
-            pair = []
-            for ft in range(2):
+            pair = {}
+            for ft in (1, 0):
                 cols = slice(ft * P, (ft + 1) * P)
                 acc = apsum.tile([P, ROWS], F32, name="acc", tag="acc")
                 mx(acc[:], 4, cols, eq[:, 0, :], es[:, 0, :], True, False)
@@ -183,16 +160,17 @@ def tile_gnnlayer_pa_t_kernel(tc, x, e_enc, W_pre, b_pre, out):
                     for q in range(4):
                         mx(acc[:, q * P : (q + 1) * P], 2 + g, cols, xr_q[:, g, b, :], xr_s[:, g, b, :], False, False)
                 mx(acc[:], 5, cols, eq[:, 1, :], es[:, 1, :], False, True)
-                pair.append(acc)
-            pl = spool.tile([P, 2, ROWS], F32, name="pl", tag="pl")
-            nc.scalar.copy(out=pl[:, 0, :], in_=pair[1][:])
-            nc.scalar.activation(out=pl[:, 1, :], in_=pair[1][:], func=ACT.Square)
+                pair[ft] = acc
+                if ft == 1:
+                    pl = spool.tile([P, 2, ROWS], F32, name="pl", tag="pl")
+                    nc.scalar.copy(out=pl[:, 0, :], in_=acc[:])
+                    nc.scalar.activation(out=pl[:, 1, :], in_=acc[:], func=ACT.Square)
+                    planes[c] = pl
             accs[c] = pair
-            planes[c] = pl
 
         def reduces(c):
             cols = slice(c * TGT, (c + 1) * TGT)
-            for ft in range(2):
+            for ft in (1, 0):
                 m = accs[c][ft][:].rearrange("p (i j) -> p i j", j=N)
                 nc.vector.tensor_reduce(out=maxs[:, ft, cols], in_=m, axis=AX.X, op=ALU.max)
                 nc.vector.tensor_reduce(out=mins[:, ft, cols], in_=m, axis=AX.X, op=ALU.min)
@@ -213,18 +191,8 @@ def tile_gnnlayer_pa_t_kernel(tc, x, e_enc, W_pre, b_pre, out):
             last = cur.rearrange("p (f i) j -> p f i j", f=2)
             nc.gpsimd.tensor_tensor(out=s12[:, :, cols], in0=last[:, :, :, 0], in1=last[:, :, :, 1], op=ALU.add)
 
-        def target_weights():
-            for s in range(2):
-                regroup_w(nc.scalar.copy, s)
-
         def target_term():
-            quantise(
-                w_grp[:, 0:2].rearrange("p s c t -> p (s c t)"),
-                2048,
-                w_q[:, 0:2].rearrange("p s c -> p (s c)"),
-                w_s[:, 0:2].rearrange("p s c -> p (s c)"),
-            )
-            tg = apsum.tile([P, 2, F], F32, name="tg", tag="acc")
+            tg = tpsum.tile([P, 2, F], F32, name="tg", tag="tp")
             for hb in range(2):
                 for g in range(2):
                     nc.tensor.matmul_mx(
@@ -236,82 +204,148 @@ def tile_gnnlayer_pa_t_kernel(tc, x, e_enc, W_pre, b_pre, out):
                         start=(g == 0),
                         stop=(g == 1),
                     )
-            nc.vector.tensor_tensor(
-                out=c_sb[:], in0=tg[:], in1=bias_bc[:].unsqueeze(1).to_broadcast([P, 2, F]), op=ALU.add
+            nc.scalar.copy(out=c_raw[:], in_=tg[:])
+
+        def target_bias():
+            nc.gpsimd.tensor_tensor(
+                out=c_sb[:], in0=c_raw[:], in1=bias_bc[:].unsqueeze(1).to_broadcast([P, 2, F]), op=ALU.add
             )
 
-        fin = {}
-
-        def finish_math(hb):
+        def finish_means(hb):
             cols = slice(hb * P, (hb + 1) * P)
             mean = fpool.tile([P, 2, P], F32, name="mean", tag="mean")
-            var = fpool.tile([P, 2, P], F32, name="var", tag="var")
-            std = fpool.tile([P, 2, P], F32, name="std", tag="std")
             msq = fpool.tile([P, P], F32, name="msq", tag="msq")
             nc.scalar.copy(out=mean[:, 0, :], in_=bst[:, cols, 1])
             nc.scalar.mul(out=mean[:, 1, :], in_=s12[:, 0, cols], mul=1.0 / N)
             nc.scalar.activation(out=msq[:], in_=s12[:, 0, cols], func=ACT.Square, scale=1.0 / N)
-            nc.vector.tensor_scalar_mul(out=var[:, 0, :], in0=bst[:, cols, 2], scalar1=1.0 / N)
-            nc.vector.scalar_tensor_tensor(
-                out=var[:, 1, :], in0=s12[:, 1, cols], scalar=1.0 / N, in1=msq[:], op0=ALU.mult, op1=ALU.subtract
-            )
-            nc.vector.tensor_scalar_max(out=var[:], in0=var[:], scalar1=0.0)
-            nc.scalar.activation(out=std[:], in_=var[:], func=ACT.Sqrt, bias=eps_t[:])
-            fin[hb] = (mean, std)
+            fin[hb] = {"mean": mean, "msq": msq}
 
-        def finish_transposes(hb):
+        def finish_variance(hb, eng):
             cols = slice(hb * P, (hb + 1) * P)
-            mean, std = fin[hb]
+            var = fpool.tile([P, 2, P], F32, name="var", tag="var")
+            eng.tensor_scalar(out=var[:, 0, :], in0=bst[:, cols, 2], scalar1=1.0 / N, scalar2=0.0, op0=ALU.mult, op1=ALU.add)
+            eng.tensor_scalar(out=var[:, 1, :], in0=s12[:, 1, cols], scalar1=1.0 / N, scalar2=0.0, op0=ALU.mult, op1=ALU.add)
+            eng.tensor_tensor(out=var[:, 1, :], in0=var[:, 1, :], in1=fin[hb]["msq"][:], op=ALU.subtract)
+            eng.tensor_scalar(out=var[:], in0=var[:], scalar1=0.0, scalar2=0.0, op0=ALU.max, op1=ALU.add)
+            fin[hb]["var"] = var
+
+        def finish_std(hb):
+            std = fpool.tile([P, 2, P], F32, name="std", tag="std")
+            nc.scalar.activation(out=std[:], in_=fin[hb]["var"][:], func=ACT.Sqrt, bias=eps_t[:])
+            fin[hb]["std"] = std
+
+        def finish_low(hb):
+            cols = slice(hb * P, (hb + 1) * P)
             f0 = tpsum.tile([P, 4, P], F32, name="f0", tag="tp")
-            f1 = tpsum.tile([P, 4, P], F32, name="f1", tag="tp")
             for ft in range(2):
-                nc.tensor.transpose(f0[:, ft, :], mean[:, ft, :], ident[:])
+                nc.tensor.transpose(f0[:, ft, :], fin[hb]["mean"][:, ft, :], ident[:])
             for ft in range(2):
                 nc.tensor.transpose(f0[:, 2 + ft, :], mins[:, ft, cols], ident[:])
+            fin[hb]["f0"] = f0
+
+        def finish_high(hb):
+            cols = slice(hb * P, (hb + 1) * P)
+            f1 = tpsum.tile([P, 4, P], F32, name="f1", tag="tp")
             for ft in range(2):
                 nc.tensor.transpose(f1[:, ft, :], maxs[:, ft, cols], ident[:])
             for ft in range(2):
-                nc.tensor.transpose(f1[:, 2 + ft, :], std[:, ft, :], ident[:])
-            fin[hb] = (f0, f1)
+                nc.tensor.transpose(f1[:, 2 + ft, :], fin[hb]["std"][:, ft, :], ident[:])
+            fin[hb]["f1"] = f1
 
-        def finish_store(hb):
-            f0, f1 = fin[hb]
-            osb = fpool.tile([P, 4, F], F32, name="osb", tag="osb")
-            shift = c_sb[:, hb, :]
+        def store_low(hb):
+            lo = fpool.tile([P, 2, F], F32, name="lo", tag="lo")
             nc.vector.tensor_tensor(
-                out=osb[:, 0:2, :],
-                in0=f0[:].rearrange("p (s f) r -> p s (f r)", f=2),
-                in1=shift.unsqueeze(1).to_broadcast([P, 2, F]),
+                out=lo[:],
+                in0=fin[hb]["f0"][:].rearrange("p (s f) r -> p s (f r)", f=2),
+                in1=c_sb[:, hb, :].unsqueeze(1).to_broadcast([P, 2, F]),
                 op=ALU.add,
             )
-            nc.vector.tensor_tensor(
-                out=osb[:, 2, :], in0=f1[:, 0:2, :].rearrange("p f r -> p (f r)"), in1=shift, op=ALU.add
-            )
-            nc.scalar.copy(out=osb[:, 3, :], in_=f1[:, 2:4, :].rearrange("p f r -> p (f r)"))
-            nc.sync.dma_start(out=out_rows[hb * P : (hb + 1) * P, :], in_=osb[:].rearrange("p s f -> p (s f)"))
+            nc.sync.dma_start(out=out_rows[hb * P : (hb + 1) * P, 0 : 2 * F], in_=lo[:].rearrange("p s f -> p (s f)"))
 
-        for n in range(-2, NCH + 1):
-            if n >= 0 and n + LOOKAHEAD < NCH:
-                load(n + LOOKAHEAD)
-            if n == 11:
-                finish_transposes(0)
-            if 0 <= n + 2 < NCH:
-                front(n + 2)
-            if n == 3:
-                target_weights()
-            if n == 5:
-                target_term()
-            if 0 <= n < NCH:
-                messages(n)
+        def store_high(hb):
+            f1 = fin[hb]["f1"]
+            hi = fpool.tile([P, 2, F], F32, name="hi", tag="hi")
+            nc.vector.tensor_tensor(
+                out=hi[:, 0, :], in0=f1[:, 0:2, :].rearrange("p f r -> p (f r)"), in1=c_sb[:, hb, :], op=ALU.add
+            )
+            nc.scalar.copy(out=hi[:, 1, :], in_=f1[:, 2:4, :].rearrange("p f r -> p (f r)"))
+            nc.sync.dma_start(out=out_rows[hb * P : (hb + 1) * P, 2 * F : 4 * F], in_=hi[:].rearrange("p s f -> p (s f)"))
+
+        nc.sync.dma_start(out=x_raw[:], in_=x.flatten_outer_dims().rearrange("(t p) k -> p t k", p=P))
+        load(0, 4)
+        load_w(2)
+        load_w(1)
+        load(1)
+        load(2)
+        load_w(0)
+        nc.sync.dma_start(out=bias_bc[:], in_=b_pre.partition_broadcast(P))
+        load(3)
+        load(4)
+
+        nc.vector.memset(eps_t[:], EPS_STD)
+        nc.vector.memset(warm[:], 1.0)
+        nc.vector.memset(x_s[:].rearrange("p g n -> p (g n)").bitcast(I32), 0)
+        nc.scalar.sqrt(warm[:], warm[:])
+        make_identity(nc, ident[:])
+        regroup_w_gpsimd(0)
+
+        for t in range(2):
+            tp = transpose_rows(x_raw[:, t, :])
+            evacuate(tp, x_grp[:, :, t * P : (t + 1) * P, :])
+        quantise(
+            x_grp[:].rearrange("p g n u -> p (g n u)").bitcast(BF16),
+            x_q[:].rearrange("p g n -> p (g n)"),
+            x_s[:].rearrange("p g n -> p (g n)"),
+        )
+        nc.vector.tensor_copy(
+            out=xr_q[:].bitcast(I32).rearrange("p g b (d j) -> p (g b) d j", d=4),
+            in_=x_q[:].bitcast(I32).rearrange("p g (b j) -> p (g b) j", j=N).unsqueeze(2).to_broadcast([P, 2 * B, 4, N]),
+        )
+        nc.vector.tensor_copy(
+            out=xr_s[:].bitcast(I32).rearrange("p g b (d j) -> p (g b) d j", d=4),
+            in_=x_s[:].bitcast(I32).rearrange("p g (b j) -> p (g b) j", j=N // 4).unsqueeze(2).to_broadcast([P, 2 * B, 4, N // 4]),
+        )
+        regroup_w_vector(2)
+        quantise_w(2)
+        front(0)
+        quantise_chunk(0)
+        regroup_w_vector(1)
+        quantise_w(1)
+
+        for n in range(0, NCH + 1):
+            if n + PRELOAD < NCH:
+                load(n + PRELOAD)
             if n == 10:
-                finish_math(0)
+                finish_means(0)
+            if n + 1 < NCH:
+                front(n + 1)
+            if n == 14:
+                finish_low(0)
+                finish_high(0)
+            if n < NCH:
+                messages(n)
+            if n == 4:
+                target_term()
+            if n == 11:
+                finish_variance(0, nc.gpsimd)
             if n == 12:
-                finish_store(0)
-            if 0 <= n + 1 < NCH:
-                quantise_chunk(n + 1)
-            if 0 <= n - 1 < NCH:
+                finish_std(0)
+            if n == 15:
+                store_low(0)
+                store_high(0)
+            if n >= 1:
                 reduces(n - 1)
                 plane_sums(n - 1)
-        finish_math(1)
-        finish_transposes(1)
-        finish_store(1)
+            if n == 6:
+                target_bias()
+            if n == 3:
+                quantise_w(0)
+            if n + 1 < NCH:
+                quantise_chunk(n + 1)
+        finish_means(1)
+        finish_low(1)
+        finish_variance(1, nc.vector)
+        finish_std(1)
+        store_low(1)
+        finish_high(1)
+        store_high(1)

@@ -33,6 +33,7 @@ def tile_gnnlayer_pa_t_kernel(tc, x, e_enc, W_pre, b_pre, out):
         epool = ctx.enter_context(tc.tile_pool(name="epool", bufs=6))
         gpool = ctx.enter_context(tc.tile_pool(name="gpool", bufs=3))
         qpool = ctx.enter_context(tc.tile_pool(name="qpool", bufs=3))
+        rpool = ctx.enter_context(tc.tile_pool(name="rpool", bufs=2))
         spool = ctx.enter_context(tc.tile_pool(name="spool", bufs=3))
         tree = ctx.enter_context(tc.tile_pool(name="tree", bufs=2))
         fpool = ctx.enter_context(tc.tile_pool(name="fpool", bufs=2))
@@ -51,8 +52,6 @@ def tile_gnnlayer_pa_t_kernel(tc, x, e_enc, W_pre, b_pre, out):
         x_grp = const.tile([P, 2, 2 * P, 2], F32, name="x_grp", align_bytes=64)
         x_q = const.tile([P, 2, 2 * P], U32, name="x_q", align_bytes=64)
         x_s = const.tile([P, 2, 2 * P], U8, name="x_s", align_bytes=64)
-        xr_q = const.tile([P, 2, B, P], U32, name="xr_q", align_bytes=64)
-        xr_s = const.tile([P, 2, B, P], U8, name="xr_s", align_bytes=64)
         bias_bc = const.tile([P, F], BF16, name="bias_bc")
         c_raw = const.tile([P, 2, F], F32, name="c_raw")
         c_sb = const.tile([P, 2, F], F32, name="c_sb")
@@ -72,6 +71,7 @@ def tile_gnnlayer_pa_t_kernel(tc, x, e_enc, W_pre, b_pre, out):
         accs = {}
         planes = {}
         fin = {}
+        sources = {}
 
         def load(c, pieces=1):
             et = epool.tile([P, 4, C], BF16, name="et", tag="et")
@@ -137,6 +137,19 @@ def tile_gnnlayer_pa_t_kernel(tc, x, e_enc, W_pre, b_pre, out):
             )
             codes[c] = (eq, es)
 
+        def repeat_sources(b):
+            xr_q = rpool.tile([P, 2, ROWS], U32, name="xr_q", tag="xr_q", align_bytes=64)
+            xr_s = rpool.tile([P, 2, ROWS], U8, name="xr_s", tag="xr_s", align_bytes=64)
+            nc.vector.tensor_copy(
+                out=xr_q[:].bitcast(I32).rearrange("p g (d j) -> p g d j", d=TGT),
+                in_=x_q[:, :, b * N : (b + 1) * N].bitcast(I32).unsqueeze(2).to_broadcast([P, 2, TGT, N]),
+            )
+            nc.vector.tensor_copy(
+                out=xr_s[:].bitcast(I32).rearrange("p g (d j) -> p g d j", d=TGT),
+                in_=x_s[:, :, b * N : (b + 1) * N].bitcast(I32).unsqueeze(2).to_broadcast([P, 2, TGT, N // 4]),
+            )
+            sources[b] = (xr_q, xr_s)
+
         def mx(out_ap, s, cols, rhs, rhs_scale, start, stop):
             nc.tensor.matmul_mx(
                 out=out_ap,
@@ -151,14 +164,14 @@ def tile_gnnlayer_pa_t_kernel(tc, x, e_enc, W_pre, b_pre, out):
         def messages(c):
             b = c // 2
             eq, es = codes[c]
+            xr_q, xr_s = sources[b]
             pair = {}
             for ft in (1, 0):
                 cols = slice(ft * P, (ft + 1) * P)
                 acc = apsum.tile([P, ROWS], F32, name="acc", tag="acc")
                 mx(acc[:], 4, cols, eq[:, 0, :], es[:, 0, :], True, False)
                 for g in range(2):
-                    for q in range(4):
-                        mx(acc[:, q * P : (q + 1) * P], 2 + g, cols, xr_q[:, g, b, :], xr_s[:, g, b, :], False, False)
+                    mx(acc[:], 2 + g, cols, xr_q[:, g, :], xr_s[:, g, :], False, False)
                 mx(acc[:], 5, cols, eq[:, 1, :], es[:, 1, :], False, True)
                 pair[ft] = acc
                 if ft == 1:
@@ -297,14 +310,7 @@ def tile_gnnlayer_pa_t_kernel(tc, x, e_enc, W_pre, b_pre, out):
             x_q[:].rearrange("p g n -> p (g n)"),
             x_s[:].rearrange("p g n -> p (g n)"),
         )
-        nc.vector.tensor_copy(
-            out=xr_q[:].bitcast(I32).rearrange("p g b (d j) -> p (g b) d j", d=4),
-            in_=x_q[:].bitcast(I32).rearrange("p g (b j) -> p (g b) j", j=N).unsqueeze(2).to_broadcast([P, 2 * B, 4, N]),
-        )
-        nc.vector.tensor_copy(
-            out=xr_s[:].bitcast(I32).rearrange("p g b (d j) -> p (g b) d j", d=4),
-            in_=x_s[:].bitcast(I32).rearrange("p g (b j) -> p (g b) j", j=N // 4).unsqueeze(2).to_broadcast([P, 2 * B, 4, N // 4]),
-        )
+        repeat_sources(0)
         regroup_w_vector(2)
         quantise_w(2)
         front(0)
@@ -340,6 +346,8 @@ def tile_gnnlayer_pa_t_kernel(tc, x, e_enc, W_pre, b_pre, out):
                 target_bias()
             if n == 3:
                 quantise_w(0)
+            if n % 2 == 1 and n + 1 < NCH:
+                repeat_sources((n + 1) // 2)
             if n + 1 < NCH:
                 quantise_chunk(n + 1)
         finish_means(1)

@@ -33,7 +33,6 @@ def tile_gnnlayer_pa_t_kernel(tc, x, e_enc, W_pre, b_pre, out):
         epool = ctx.enter_context(tc.tile_pool(name="epool", bufs=6))
         gpool = ctx.enter_context(tc.tile_pool(name="gpool", bufs=3))
         qpool = ctx.enter_context(tc.tile_pool(name="qpool", bufs=3))
-        rpool = ctx.enter_context(tc.tile_pool(name="rpool", bufs=2))
         spool = ctx.enter_context(tc.tile_pool(name="spool", bufs=3))
         tree = ctx.enter_context(tc.tile_pool(name="tree", bufs=2))
         fpool = ctx.enter_context(tc.tile_pool(name="fpool", bufs=2))
@@ -52,10 +51,12 @@ def tile_gnnlayer_pa_t_kernel(tc, x, e_enc, W_pre, b_pre, out):
         x_grp = const.tile([P, 2, 2 * P, 2], F32, name="x_grp", align_bytes=64)
         x_q = const.tile([P, 2, 2 * P], U32, name="x_q", align_bytes=64)
         x_s = const.tile([P, 2, 2 * P], U8, name="x_s", align_bytes=64)
+        xr_q = const.tile([P, B, 2, P], U32, name="xr_q", align_bytes=64)
+        xr_s = const.tile([P, B, 2, P], U8, name="xr_s", align_bytes=64)
         bias_bc = const.tile([P, F], BF16, name="bias_bc")
         c_raw = const.tile([P, 2, F], F32, name="c_raw")
         c_sb = const.tile([P, 2, F], F32, name="c_sb")
-        bst = const.tile([P, B * N, 3], F32, name="bst")
+        bst = const.tile([P, 2, B * N, 3], F32, name="bst")
         s12 = const.tile([P, 2, B * N], F32, name="s12")
         mins = const.tile([P, 2, B * N], F32, name="mins")
         maxs = const.tile([P, 2, B * N], F32, name="maxs")
@@ -71,7 +72,6 @@ def tile_gnnlayer_pa_t_kernel(tc, x, e_enc, W_pre, b_pre, out):
         accs = {}
         planes = {}
         fin = {}
-        sources = {}
 
         def load(c, pieces=1):
             et = epool.tile([P, 4, C], BF16, name="et", tag="et")
@@ -137,19 +137,6 @@ def tile_gnnlayer_pa_t_kernel(tc, x, e_enc, W_pre, b_pre, out):
             )
             codes[c] = (eq, es)
 
-        def repeat_sources(b):
-            xr_q = rpool.tile([P, 2, ROWS], U32, name="xr_q", tag="xr_q", align_bytes=64)
-            xr_s = rpool.tile([P, 2, ROWS], U8, name="xr_s", tag="xr_s", align_bytes=64)
-            nc.vector.tensor_copy(
-                out=xr_q[:].bitcast(I32).rearrange("p g (d j) -> p g d j", d=TGT),
-                in_=x_q[:, :, b * N : (b + 1) * N].bitcast(I32).unsqueeze(2).to_broadcast([P, 2, TGT, N]),
-            )
-            nc.vector.tensor_copy(
-                out=xr_s[:].bitcast(I32).rearrange("p g (d j) -> p g d j", d=TGT),
-                in_=x_s[:, :, b * N : (b + 1) * N].bitcast(I32).unsqueeze(2).to_broadcast([P, 2, TGT, N // 4]),
-            )
-            sources[b] = (xr_q, xr_s)
-
         def mx(out_ap, s, cols, rhs, rhs_scale, start, stop):
             nc.tensor.matmul_mx(
                 out=out_ap,
@@ -164,17 +151,17 @@ def tile_gnnlayer_pa_t_kernel(tc, x, e_enc, W_pre, b_pre, out):
         def messages(c):
             b = c // 2
             eq, es = codes[c]
-            xr_q, xr_s = sources[b]
             pair = {}
             for ft in (1, 0):
                 cols = slice(ft * P, (ft + 1) * P)
                 acc = apsum.tile([P, ROWS], F32, name="acc", tag="acc")
                 mx(acc[:], 4, cols, eq[:, 0, :], es[:, 0, :], True, False)
                 for g in range(2):
-                    mx(acc[:], 2 + g, cols, xr_q[:, g, :], xr_s[:, g, :], False, False)
+                    for q in range(4):
+                        mx(acc[:, q * P : (q + 1) * P], 2 + g, cols, xr_q[:, b, g, :], xr_s[:, b, g, :], False, False)
                 mx(acc[:], 5, cols, eq[:, 1, :], es[:, 1, :], False, True)
                 pair[ft] = acc
-                if ft == 1:
+                if ft == 1 and c < NCH - 1:
                     pl = spool.tile([P, 2, ROWS], F32, name="pl", tag="pl")
                     nc.scalar.copy(out=pl[:, 0, :], in_=acc[:])
                     nc.scalar.activation(out=pl[:, 1, :], in_=acc[:], func=ACT.Square)
@@ -187,10 +174,10 @@ def tile_gnnlayer_pa_t_kernel(tc, x, e_enc, W_pre, b_pre, out):
                 m = accs[c][ft][:].rearrange("p (i j) -> p i j", j=N)
                 nc.vector.tensor_reduce(out=maxs[:, ft, cols], in_=m, axis=AX.X, op=ALU.max)
                 nc.vector.tensor_reduce(out=mins[:, ft, cols], in_=m, axis=AX.X, op=ALU.min)
-                if ft == 0:
+                if ft == 0 or c == NCH - 1:
                     for i in range(0, TGT, 2):
                         nc.vector.bn_stats(
-                            out=bst[:, c * TGT + i : c * TGT + i + 2, :].rearrange("p m s -> p (m s)"),
+                            out=bst[:, ft, c * TGT + i : c * TGT + i + 2, :].rearrange("p m s -> p (m s)"),
                             in_=m[:, i : i + 2, :].rearrange("p m j -> p j m"),
                         )
 
@@ -224,65 +211,79 @@ def tile_gnnlayer_pa_t_kernel(tc, x, e_enc, W_pre, b_pre, out):
                 out=c_sb[:], in0=c_raw[:], in1=bias_bc[:].unsqueeze(1).to_broadcast([P, 2, F]), op=ALU.add
             )
 
-        def finish_means(hb):
+        def finish_tiles(hb):
+            fin[hb] = {
+                "mean": fpool.tile([P, 2, P], F32, name="mean", tag="mean"),
+                "var": fpool.tile([P, 2, P], F32, name="var", tag="var"),
+                "msq": fpool.tile([P, P], F32, name="msq", tag="msq"),
+            }
+
+        def stats_from_bn(eng, hb, ft, lo, hi):
+            cols = slice(hb * P + lo, hb * P + hi)
+            eng.tensor_scalar(
+                out=fin[hb]["var"][:, ft, lo:hi], in0=bst[:, ft, cols, 2], scalar1=1.0 / N, scalar2=0.0, op0=ALU.mult, op1=ALU.max
+            )
+            eng.tensor_scalar(
+                out=fin[hb]["mean"][:, ft, lo:hi], in0=bst[:, ft, cols, 1], scalar1=1.0, scalar2=0.0, op0=ALU.mult, op1=ALU.add
+            )
+
+        def stats_from_sums(eng, hb, lo, hi):
+            cols = slice(hb * P + lo, hb * P + hi)
+            mean = fin[hb]["mean"][:, 1, lo:hi]
+            var = fin[hb]["var"][:, 1, lo:hi]
+            msq = fin[hb]["msq"][:, lo:hi]
+            eng.tensor_scalar(out=mean, in0=s12[:, 0, cols], scalar1=1.0 / N, scalar2=0.0, op0=ALU.mult, op1=ALU.add)
+            eng.tensor_tensor(out=msq, in0=mean, in1=mean, op=ALU.mult)
+            eng.tensor_scalar(out=var, in0=s12[:, 1, cols], scalar1=1.0 / N, scalar2=0.0, op0=ALU.mult, op1=ALU.add)
+            eng.tensor_tensor(out=var, in0=var, in1=msq, op=ALU.subtract)
+            eng.tensor_scalar(out=var, in0=var, scalar1=0.0, scalar2=0.0, op0=ALU.max, op1=ALU.add)
+
+        def finish_transposes(hb):
             cols = slice(hb * P, (hb + 1) * P)
-            mean = fpool.tile([P, 2, P], F32, name="mean", tag="mean")
-            msq = fpool.tile([P, P], F32, name="msq", tag="msq")
-            nc.scalar.copy(out=mean[:, 0, :], in_=bst[:, cols, 1])
-            nc.scalar.mul(out=mean[:, 1, :], in_=s12[:, 0, cols], mul=1.0 / N)
-            nc.scalar.activation(out=msq[:], in_=s12[:, 0, cols], func=ACT.Square, scale=1.0 / N)
-            fin[hb] = {"mean": mean, "msq": msq}
-
-        def finish_variance(hb, eng):
-            cols = slice(hb * P, (hb + 1) * P)
-            var = fpool.tile([P, 2, P], F32, name="var", tag="var")
-            eng.tensor_scalar(out=var[:, 0, :], in0=bst[:, cols, 2], scalar1=1.0 / N, scalar2=0.0, op0=ALU.mult, op1=ALU.add)
-            eng.tensor_scalar(out=var[:, 1, :], in0=s12[:, 1, cols], scalar1=1.0 / N, scalar2=0.0, op0=ALU.mult, op1=ALU.add)
-            eng.tensor_tensor(out=var[:, 1, :], in0=var[:, 1, :], in1=fin[hb]["msq"][:], op=ALU.subtract)
-            eng.tensor_scalar(out=var[:], in0=var[:], scalar1=0.0, scalar2=0.0, op0=ALU.max, op1=ALU.add)
-            fin[hb]["var"] = var
-
-        def finish_std(hb):
-            std = fpool.tile([P, 2, P], F32, name="std", tag="std")
-            nc.scalar.activation(out=std[:], in_=fin[hb]["var"][:], func=ACT.Sqrt, bias=eps_t[:])
-            fin[hb]["std"] = std
-
-        def finish_low(hb):
-            cols = slice(hb * P, (hb + 1) * P)
-            f0 = tpsum.tile([P, 4, P], F32, name="f0", tag="tp")
+            fv = tpsum.tile([P, 2, P], F32, name="fv", tag="tp")
+            fx = tpsum.tile([P, 2, P], F32, name="fx", tag="tp")
+            fm = tpsum.tile([P, 4, P], F32, name="fm", tag="tp")
             for ft in range(2):
-                nc.tensor.transpose(f0[:, ft, :], fin[hb]["mean"][:, ft, :], ident[:])
+                nc.tensor.transpose(fv[:, ft, :], fin[hb]["var"][:, ft, :], ident[:])
             for ft in range(2):
-                nc.tensor.transpose(f0[:, 2 + ft, :], mins[:, ft, cols], ident[:])
-            fin[hb]["f0"] = f0
+                nc.tensor.transpose(fx[:, ft, :], maxs[:, ft, cols], ident[:])
+            for ft in range(2):
+                nc.tensor.transpose(fm[:, ft, :], fin[hb]["mean"][:, ft, :], ident[:])
+            for ft in range(2):
+                nc.tensor.transpose(fm[:, 2 + ft, :], mins[:, ft, cols], ident[:])
+            fin[hb]["fv"] = fv
+            fin[hb]["fx"] = fx
+            fin[hb]["fm"] = fm
 
-        def finish_high(hb):
-            cols = slice(hb * P, (hb + 1) * P)
-            f1 = tpsum.tile([P, 4, P], F32, name="f1", tag="tp")
-            for ft in range(2):
-                nc.tensor.transpose(f1[:, ft, :], maxs[:, ft, cols], ident[:])
-            for ft in range(2):
-                nc.tensor.transpose(f1[:, 2 + ft, :], fin[hb]["std"][:, ft, :], ident[:])
-            fin[hb]["f1"] = f1
-
-        def store_low(hb):
+        def finish_stores(hb):
+            rows = slice(hb * P, (hb + 1) * P)
+            hi = fpool.tile([P, 2, F], F32, name="hi", tag="hi")
             lo = fpool.tile([P, 2, F], F32, name="lo", tag="lo")
+            nc.scalar.activation(
+                out=hi[:, 1, :], in_=fin[hb]["fv"][:].rearrange("p f r -> p (f r)"), func=ACT.Sqrt, bias=eps_t[:]
+            )
+            nc.vector.tensor_tensor(
+                out=hi[:, 0, :], in0=fin[hb]["fx"][:].rearrange("p f r -> p (f r)"), in1=c_sb[:, hb, :], op=ALU.add
+            )
+            nc.sync.dma_start(out=out_rows[rows, 2 * F : 4 * F], in_=hi[:].rearrange("p s f -> p (s f)"))
             nc.vector.tensor_tensor(
                 out=lo[:],
-                in0=fin[hb]["f0"][:].rearrange("p (s f) r -> p s (f r)", f=2),
+                in0=fin[hb]["fm"][:].rearrange("p (s f) r -> p s (f r)", f=2),
                 in1=c_sb[:, hb, :].unsqueeze(1).to_broadcast([P, 2, F]),
                 op=ALU.add,
             )
-            nc.sync.dma_start(out=out_rows[hb * P : (hb + 1) * P, 0 : 2 * F], in_=lo[:].rearrange("p s f -> p (s f)"))
+            nc.sync.dma_start(out=out_rows[rows, 0 : 2 * F], in_=lo[:].rearrange("p s f -> p (s f)"))
 
-        def store_high(hb):
-            f1 = fin[hb]["f1"]
-            hi = fpool.tile([P, 2, F], F32, name="hi", tag="hi")
-            nc.vector.tensor_tensor(
-                out=hi[:, 0, :], in0=f1[:, 0:2, :].rearrange("p f r -> p (f r)"), in1=c_sb[:, hb, :], op=ALU.add
-            )
-            nc.scalar.copy(out=hi[:, 1, :], in_=f1[:, 2:4, :].rearrange("p f r -> p (f r)"))
-            nc.sync.dma_start(out=out_rows[hb * P : (hb + 1) * P, 2 * F : 4 * F], in_=hi[:].rearrange("p s f -> p (s f)"))
+        def repeat_sources(b0, b1):
+            for g in range(2):
+                nc.vector.tensor_copy(
+                    out=xr_q[:, b0:b1, g, :].bitcast(I32).rearrange("p b (d j) -> p b d j", d=4),
+                    in_=x_q[:, g, b0 * N : b1 * N].bitcast(I32).rearrange("p (b j) -> p b j", j=N).unsqueeze(2).to_broadcast([P, b1 - b0, 4, N]),
+                )
+                nc.vector.tensor_copy(
+                    out=xr_s[:, b0:b1, g, :].bitcast(I32).rearrange("p b (d j) -> p b d j", d=4),
+                    in_=x_s[:, g, b0 * N : b1 * N].bitcast(I32).rearrange("p (b j) -> p b j", j=N // 4).unsqueeze(2).to_broadcast([P, b1 - b0, 4, N // 4]),
+                )
 
         nc.sync.dma_start(out=x_raw[:], in_=x.flatten_outer_dims().rearrange("(t p) k -> p t k", p=P))
         load(0, 4)
@@ -310,50 +311,46 @@ def tile_gnnlayer_pa_t_kernel(tc, x, e_enc, W_pre, b_pre, out):
             x_q[:].rearrange("p g n -> p (g n)"),
             x_s[:].rearrange("p g n -> p (g n)"),
         )
-        repeat_sources(0)
+        repeat_sources(0, 1)
         regroup_w_vector(2)
         quantise_w(2)
-        front(0)
-        quantise_chunk(0)
-        regroup_w_vector(1)
-        quantise_w(1)
 
-        for n in range(0, NCH + 1):
-            if n + PRELOAD < NCH:
+        for n in range(-2, NCH + 1):
+            if 0 <= n and n + PRELOAD < NCH:
                 load(n + PRELOAD)
-            if n == 10:
-                finish_means(0)
-            if n + 1 < NCH:
-                front(n + 1)
-            if n == 14:
-                finish_low(0)
-                finish_high(0)
-            if n < NCH:
+            if n + 2 < NCH:
+                front(n + 2)
+            if n == 13:
+                finish_transposes(0)
+            if 0 <= n < NCH:
                 messages(n)
             if n == 4:
                 target_term()
-            if n == 11:
-                finish_variance(0, nc.gpsimd)
-            if n == 12:
-                finish_std(0)
-            if n == 15:
-                store_low(0)
-                store_high(0)
-            if n >= 1:
-                reduces(n - 1)
-                plane_sums(n - 1)
-            if n == 6:
-                target_bias()
+            if n == 14:
+                finish_stores(0)
             if n == 3:
                 quantise_w(0)
-            if n % 2 == 1 and n + 1 < NCH:
-                repeat_sources((n + 1) // 2)
-            if n + 1 < NCH:
+            if 0 <= n + 1 < NCH:
                 quantise_chunk(n + 1)
-        finish_means(1)
-        finish_low(1)
-        finish_variance(1, nc.vector)
-        finish_std(1)
-        store_low(1)
-        finish_high(1)
-        store_high(1)
+            if n == -1:
+                regroup_w_vector(1)
+                quantise_w(1)
+                repeat_sources(1, B)
+            if n >= 1:
+                reduces(n - 1)
+                if n - 1 < NCH - 1:
+                    plane_sums(n - 1)
+            if n == 6:
+                target_bias()
+            if n == 10:
+                finish_tiles(0)
+                stats_from_bn(nc.gpsimd, 0, 0, 0, P)
+                stats_from_sums(nc.gpsimd, 0, 0, P)
+            if n == 15:
+                finish_tiles(1)
+                stats_from_bn(nc.gpsimd, 1, 0, 0, P - TGT)
+                stats_from_sums(nc.gpsimd, 1, 0, P - TGT)
+        stats_from_bn(nc.vector, 1, 1, P - TGT, P)
+        stats_from_bn(nc.vector, 1, 0, P - TGT, P)
+        finish_transposes(1)
+        finish_stores(1)

@@ -24,6 +24,7 @@ NCH = B * N * N // ROWS
 TGT = ROWS // N
 FLOPS = 2 * C * F * (B * N * N + 2 * B * N)
 PRELOAD = 5
+SUMMED = NCH - 2
 
 
 def tile_gnnlayer_pa_t_kernel(tc, x, e_enc, W_pre, b_pre, out):
@@ -71,6 +72,7 @@ def tile_gnnlayer_pa_t_kernel(tc, x, e_enc, W_pre, b_pre, out):
         codes = {}
         accs = {}
         planes = {}
+        halves = {}
         fin = {}
 
         def load(c, pieces=1):
@@ -161,11 +163,12 @@ def tile_gnnlayer_pa_t_kernel(tc, x, e_enc, W_pre, b_pre, out):
                         mx(acc[:, q * P : (q + 1) * P], 2 + g, cols, xr_q[:, b, g, :], xr_s[:, b, g, :], False, False)
                 mx(acc[:], 5, cols, eq[:, 1, :], es[:, 1, :], False, True)
                 pair[ft] = acc
-                if ft == 1 and c < NCH - 1:
-                    pl = spool.tile([P, 2, ROWS], F32, name="pl", tag="pl")
-                    nc.scalar.copy(out=pl[:, 0, :], in_=acc[:])
-                    nc.scalar.activation(out=pl[:, 1, :], in_=acc[:], func=ACT.Square)
-                    planes[c] = pl
+                if ft == 1 and c < SUMMED:
+                    if c % 2 == 0:
+                        planes[c // 2] = spool.tile([P, 2, 2, ROWS], F32, name="pl", tag="pl")
+                    pl = planes[c // 2]
+                    nc.scalar.copy(out=pl[:, 0, c % 2, :], in_=acc[:])
+                    nc.scalar.activation(out=pl[:, 1, c % 2, :], in_=acc[:], func=ACT.Square)
             accs[c] = pair
 
         def reduces(c):
@@ -174,18 +177,26 @@ def tile_gnnlayer_pa_t_kernel(tc, x, e_enc, W_pre, b_pre, out):
                 m = accs[c][ft][:].rearrange("p (i j) -> p i j", j=N)
                 nc.vector.tensor_reduce(out=maxs[:, ft, cols], in_=m, axis=AX.X, op=ALU.max)
                 nc.vector.tensor_reduce(out=mins[:, ft, cols], in_=m, axis=AX.X, op=ALU.min)
-                if ft == 0 or c == NCH - 1:
+                if ft == 0 or c >= SUMMED:
                     for i in range(0, TGT, 2):
                         nc.vector.bn_stats(
                             out=bst[:, ft, c * TGT + i : c * TGT + i + 2, :].rearrange("p m s -> p (m s)"),
                             in_=m[:, i : i + 2, :].rearrange("p m j -> p j m"),
                         )
 
-        def plane_sums(c):
-            cols = slice(c * TGT, (c + 1) * TGT)
-            cur = planes[c][:].rearrange("p f (i j) -> p (f i) j", j=N)
-            for width in (16, 8, 4, 2):
-                nxt = tree.tile([P, 2 * TGT, width], F32, name="lvl%d" % width, tag="lvl%d" % width)
+        def first_level(c):
+            if c % 2 == 0:
+                halves[c // 2] = tree.tile([P, 2, 2, TGT, N // 2], F32, name="lvl16", tag="lvl16")
+            src = planes[c // 2][:, :, c % 2, :].rearrange("p f (i j) -> p f i j", j=N)
+            nc.gpsimd.tensor_tensor(
+                out=halves[c // 2][:, :, c % 2, :, :], in0=src[:, :, :, 0 : N // 2], in1=src[:, :, :, N // 2 : N], op=ALU.add
+            )
+
+        def upper_levels(pair):
+            cols = slice(2 * pair * TGT, 2 * (pair + 1) * TGT)
+            cur = halves[pair][:].rearrange("p f c i j -> p (f c i) j")
+            for width in (8, 4, 2):
+                nxt = tree.tile([P, 4 * TGT, width], F32, name="lvl%d" % width, tag="lvl%d" % width)
                 nc.gpsimd.tensor_tensor(out=nxt[:], in0=cur[:, :, 0:width], in1=cur[:, :, width : 2 * width], op=ALU.add)
                 cur = nxt[:]
             last = cur.rearrange("p (f i) j -> p f i j", f=2)
@@ -218,25 +229,33 @@ def tile_gnnlayer_pa_t_kernel(tc, x, e_enc, W_pre, b_pre, out):
                 "msq": fpool.tile([P, P], F32, name="msq", tag="msq"),
             }
 
-        def stats_from_bn(eng, hb, ft, lo, hi):
-            cols = slice(hb * P + lo, hb * P + hi)
-            eng.tensor_scalar(
-                out=fin[hb]["var"][:, ft, lo:hi], in0=bst[:, ft, cols, 2], scalar1=1.0 / N, scalar2=0.0, op0=ALU.mult, op1=ALU.max
-            )
-            eng.tensor_scalar(
-                out=fin[hb]["mean"][:, ft, lo:hi], in0=bst[:, ft, cols, 1], scalar1=1.0, scalar2=0.0, op0=ALU.mult, op1=ALU.add
+        def means_of_summed(hb, width):
+            cols = slice(hb * P, hb * P + width)
+            nc.scalar.copy(out=fin[hb]["mean"][:, 0, 0:width], in_=bst[:, 0, cols, 1])
+            nc.scalar.mul(out=fin[hb]["mean"][:, 1, 0:width], in_=s12[:, 0, cols], mul=1.0 / N)
+            nc.scalar.activation(out=fin[hb]["msq"][:, 0:width], in_=s12[:, 0, cols], func=ACT.Square, scale=1.0 / N)
+
+        def variances_of_summed(hb, width):
+            cols = slice(hb * P, hb * P + width)
+            nc.vector.tensor_scalar_mul(out=fin[hb]["var"][:, 0, 0:width], in0=bst[:, 0, cols, 2], scalar1=1.0 / N)
+            nc.vector.scalar_tensor_tensor(
+                out=fin[hb]["var"][:, 1, 0:width],
+                in0=s12[:, 1, cols],
+                scalar=1.0 / N,
+                in1=fin[hb]["msq"][:, 0:width],
+                op0=ALU.mult,
+                op1=ALU.subtract,
             )
 
-        def stats_from_sums(eng, hb, lo, hi):
-            cols = slice(hb * P + lo, hb * P + hi)
-            mean = fin[hb]["mean"][:, 1, lo:hi]
-            var = fin[hb]["var"][:, 1, lo:hi]
-            msq = fin[hb]["msq"][:, lo:hi]
-            eng.tensor_scalar(out=mean, in0=s12[:, 0, cols], scalar1=1.0 / N, scalar2=0.0, op0=ALU.mult, op1=ALU.add)
-            eng.tensor_tensor(out=msq, in0=mean, in1=mean, op=ALU.mult)
-            eng.tensor_scalar(out=var, in0=s12[:, 1, cols], scalar1=1.0 / N, scalar2=0.0, op0=ALU.mult, op1=ALU.add)
-            eng.tensor_tensor(out=var, in0=var, in1=msq, op=ALU.subtract)
-            eng.tensor_scalar(out=var, in0=var, scalar1=0.0, scalar2=0.0, op0=ALU.max, op1=ALU.add)
+        def variances_of_rest(hb, width):
+            if width < P:
+                cols = slice(hb * P + width, (hb + 1) * P)
+                nc.vector.tensor_scalar_mul(out=fin[hb]["var"][:, :, width:P], in0=bst[:, :, cols, 2], scalar1=1.0 / N)
+            nc.vector.tensor_scalar_max(out=fin[hb]["var"][:], in0=fin[hb]["var"][:], scalar1=0.0)
+
+        def means_of_rest(hb, width):
+            cols = slice(hb * P + width, (hb + 1) * P)
+            nc.vector.tensor_copy(out=fin[hb]["mean"][:, :, width:P], in_=bst[:, :, cols, 1])
 
         def finish_transposes(hb):
             cols = slice(hb * P, (hb + 1) * P)
@@ -315,9 +334,13 @@ def tile_gnnlayer_pa_t_kernel(tc, x, e_enc, W_pre, b_pre, out):
         regroup_w_vector(2)
         quantise_w(2)
 
+        LAST = P - 2 * TGT
         for n in range(-2, NCH + 1):
             if 0 <= n and n + PRELOAD < NCH:
                 load(n + PRELOAD)
+            if n == 11:
+                finish_tiles(0)
+                means_of_summed(0, P)
             if n + 2 < NCH:
                 front(n + 2)
             if n == 13:
@@ -326,6 +349,9 @@ def tile_gnnlayer_pa_t_kernel(tc, x, e_enc, W_pre, b_pre, out):
                 messages(n)
             if n == 4:
                 target_term()
+            if n == 12:
+                variances_of_summed(0, P)
+                variances_of_rest(0, P)
             if n == 14:
                 finish_stores(0)
             if n == 3:
@@ -336,21 +362,19 @@ def tile_gnnlayer_pa_t_kernel(tc, x, e_enc, W_pre, b_pre, out):
                 regroup_w_vector(1)
                 quantise_w(1)
                 repeat_sources(1, B)
+            if n == 16:
+                finish_tiles(1)
+                means_of_summed(1, LAST)
+                variances_of_summed(1, LAST)
             if n >= 1:
                 reduces(n - 1)
-                if n - 1 < NCH - 1:
-                    plane_sums(n - 1)
+                if n - 1 < SUMMED:
+                    first_level(n - 1)
+                    if (n - 1) % 2 == 1:
+                        upper_levels((n - 1) // 2)
             if n == 6:
                 target_bias()
-            if n == 10:
-                finish_tiles(0)
-                stats_from_bn(nc.gpsimd, 0, 0, 0, P)
-                stats_from_sums(nc.gpsimd, 0, 0, P)
-            if n == 15:
-                finish_tiles(1)
-                stats_from_bn(nc.gpsimd, 1, 0, 0, P - TGT)
-                stats_from_sums(nc.gpsimd, 1, 0, P - TGT)
-        stats_from_bn(nc.vector, 1, 1, P - TGT, P)
-        stats_from_bn(nc.vector, 1, 0, P - TGT, P)
+        variances_of_rest(1, LAST)
+        means_of_rest(1, LAST)
         finish_transposes(1)
         finish_stores(1)

from contextlib import ExitStack

import concourse.mybir as mybir
from concourse.masks import make_identity

F32 = mybir.dt.float32
BF16 = mybir.dt.bfloat16
I32 = mybir.dt.int32
U32 = mybir.dt.uint32
U8 = mybir.dt.uint8
FP8X4 = mybir.dt.float8_e4m3fn_x4
ALU = mybir.AluOpType
ACT = mybir.ActivationFunctionType
AX = mybir.AxisListType

P = 128
B = 8
N = 32
C = 1024
F = 256
EPS_STD = 1e-5
ROWS = 512
NCH = B * N * N // ROWS
TGT = ROWS // N
FLOPS = 2 * C * F * (B * N * N + 2 * B * N)
PRELOAD = 5
SUMMED = NCH - 2


def tile_gnnlayer_pa_t_kernel(tc, x, e_enc, W_pre, b_pre, out):
    nc = tc.nc
    with ExitStack() as ctx:
        const = ctx.enter_context(tc.tile_pool(name="const", bufs=1))
        epool = ctx.enter_context(tc.tile_pool(name="epool", bufs=6))
        gpool = ctx.enter_context(tc.tile_pool(name="gpool", bufs=3))
        qpool = ctx.enter_context(tc.tile_pool(name="qpool", bufs=3))
        spool = ctx.enter_context(tc.tile_pool(name="spool", bufs=3))
        tree = ctx.enter_context(tc.tile_pool(name="tree", bufs=2))
        fpool = ctx.enter_context(tc.tile_pool(name="fpool", bufs=2))
        tpsum = ctx.enter_context(tc.psum_pool(name="tpsum", bufs=4))
        apsum = ctx.enter_context(tc.psum_pool(name="apsum", bufs=4))
        ctx.enter_context(tc.manual_schedule())

        eps_t = const.tile([P, 1], F32, name="eps_t")
        warm = const.tile([P, 1], F32, name="warm")
        ident = const.tile([P, P], F32, name="ident")
        w_raw = const.tile([P, 12, 2, F], BF16, name="w_raw")
        w_grp = const.tile([P, 6, F, 4], BF16, name="w_grp", align_bytes=64)
        w_q = const.tile([P, 6, F], U32, name="w_q", align_bytes=64)
        w_s = const.tile([P, 6, F], U8, name="w_s", align_bytes=64)
        x_raw = const.tile([P, 2, C], BF16, name="x_raw")
        x_grp = const.tile([P, 2, 2 * P, 2], F32, name="x_grp", align_bytes=64)
        x_q = const.tile([P, 2, 2 * P], U32, name="x_q", align_bytes=64)
        x_s = const.tile([P, 2, 2 * P], U8, name="x_s", align_bytes=64)
        xr_q = const.tile([P, B, 2, P], U32, name="xr_q", align_bytes=64)
        xr_s = const.tile([P, B, 2, P], U8, name="xr_s", align_bytes=64)
        bias_bc = const.tile([P, F], BF16, name="bias_bc")
        c_raw = const.tile([P, 2, F], F32, name="c_raw")
        c_sb = const.tile([P, 2, F], F32, name="c_sb")
        bst = const.tile([P, 2, B * N, 3], F32, name="bst")
        s12 = const.tile([P, 2, B * N], F32, name="s12")
        mins = const.tile([P, 2, B * N], F32, name="mins")
        maxs = const.tile([P, 2, B * N], F32, name="maxs")

        w_view = W_pre.rearrange("(s q e) c -> q s e c", q=P, e=2)
        w_rows = w_raw[:].rearrange("p (s u) e c -> p s (u e) c", u=2)
        e_view = e_enc.flatten_outer_dims().rearrange("(c t p) k -> c p t k", t=4, p=P)
        out_rows = out.flatten_outer_dims()

        ets = {}
        grps = {}
        codes = {}
        accs = {}
        planes = {}
        halves = {}
        fin = {}

        def load(c, pieces=1):
            et = epool.tile([P, 4, C], BF16, name="et", tag="et")
            step = 4 // pieces
            for t in range(0, 4, step):
                nc.sync.dma_start(out=et[:, t : t + step, :], in_=e_view[c][:, t : t + step, :])
            ets[c] = et

        def load_w(block):
            nc.sync.dma_start(out=w_raw[:, 4 * block : 4 * block + 4], in_=w_view[:, 4 * block : 4 * block + 4])

        def transpose_rows(rows):
            tp = tpsum.tile([P, 4, P], F32, name="tp", tag="tp")
            words = rows.bitcast(F32)
            for a in range(4):
                nc.tensor.transpose(tp[:, a, :], words[:, a * P : (a + 1) * P], ident[:])
            return tp

        def evacuate(tp, dst):
            nc.scalar.copy(out=dst, in_=tp[:].rearrange("p (g u) r -> p g r u", u=2))

        def quantise(src, q_ap, s_ap):
            nc.vector.quantize_mx(out=q_ap.bitcast(FP8X4), scales=s_ap, in_=src)

        def quantise_w(block):
            lo = 2 * block
            quantise(
                w_grp[:, lo : lo + 2].rearrange("p s c t -> p (s c t)"),
                w_q[:, lo : lo + 2].rearrange("p s c -> p (s c)"),
                w_s[:, lo : lo + 2].rearrange("p s c -> p (s c)"),
            )

        def regroup_views(s):
            return (
                w_grp[:, s].rearrange("p (c i) t -> p c t i", i=4),
                w_rows[:, s].rearrange("p t (c i) -> p c t i", i=4),
            )

        def regroup_w_vector(block):
            for s in (2 * block, 2 * block + 1):
                dst, src = regroup_views(s)
                nc.vector.tensor_copy(out=dst, in_=src)

        def regroup_w_gpsimd(block):
            for s in (2 * block, 2 * block + 1):
                dst, src = regroup_views(s)
                nc.gpsimd.tensor_scalar(out=dst, in0=src, scalar1=1.0, scalar2=0.0, op0=ALU.mult, op1=ALU.add)

        def front(c):
            grp = gpool.tile([P, 2, ROWS, 2], F32, name="grp", tag="grp", align_bytes=64)
            for t in range(4):
                tp = transpose_rows(ets[c][:, t, :])
                evacuate(tp, grp[:, :, t * P : (t + 1) * P, :])
            grps[c] = grp

        def quantise_chunk(c):
            eq = qpool.tile([P, 2, ROWS], U32, name="eq", tag="eq", align_bytes=64)
            es = qpool.tile([P, 2, ROWS], U8, name="es", tag="es", align_bytes=64)
            quantise(
                grps[c][:].rearrange("p g n u -> p (g n u)").bitcast(BF16),
                eq[:].rearrange("p g n -> p (g n)"),
                es[:].rearrange("p g n -> p (g n)"),
            )
            codes[c] = (eq, es)

        def mx(out_ap, s, cols, rhs, rhs_scale, start, stop):
            nc.tensor.matmul_mx(
                out=out_ap,
                lhsT=w_q[:, s, cols].bitcast(FP8X4),
                lhsT_scale=w_s[:, s, cols],
                rhs=rhs.bitcast(FP8X4),
                rhs_scale=rhs_scale,
                start=start,
                stop=stop,
            )

        def messages(c):
            b = c // 2
            eq, es = codes[c]
            pair = {}
            for ft in (1, 0):
                cols = slice(ft * P, (ft + 1) * P)
                acc = apsum.tile([P, ROWS], F32, name="acc", tag="acc")
                mx(acc[:], 4, cols, eq[:, 0, :], es[:, 0, :], True, False)
                for g in range(2):
                    for q in range(4):
                        mx(acc[:, q * P : (q + 1) * P], 2 + g, cols, xr_q[:, b, g, :], xr_s[:, b, g, :], False, False)
                mx(acc[:], 5, cols, eq[:, 1, :], es[:, 1, :], False, True)
                pair[ft] = acc
                if ft == 1 and c < SUMMED:
                    if c % 2 == 0:
                        planes[c // 2] = spool.tile([P, 2, 2, ROWS], F32, name="pl", tag="pl")
                    pl = planes[c // 2]
                    nc.scalar.copy(out=pl[:, 0, c % 2, :], in_=acc[:])
                    nc.scalar.activation(out=pl[:, 1, c % 2, :], in_=acc[:], func=ACT.Square)
            accs[c] = pair

        def reduces(c):
            cols = slice(c * TGT, (c + 1) * TGT)
            for ft in (1, 0):
                m = accs[c][ft][:].rearrange("p (i j) -> p i j", j=N)
                nc.vector.tensor_reduce(out=maxs[:, ft, cols], in_=m, axis=AX.X, op=ALU.max)
                nc.vector.tensor_reduce(out=mins[:, ft, cols], in_=m, axis=AX.X, op=ALU.min)
                if ft == 0 or c >= SUMMED:
                    for i in range(0, TGT, 2):
                        nc.vector.bn_stats(
                            out=bst[:, ft, c * TGT + i : c * TGT + i + 2, :].rearrange("p m s -> p (m s)"),
                            in_=m[:, i : i + 2, :].rearrange("p m j -> p j m"),
                        )

        def first_level(c):
            if c % 2 == 0:
                halves[c // 2] = tree.tile([P, 2, 2, TGT, N // 2], F32, name="lvl16", tag="lvl16")
            src = planes[c // 2][:, :, c % 2, :].rearrange("p f (i j) -> p f i j", j=N)
            nc.gpsimd.tensor_tensor(
                out=halves[c // 2][:, :, c % 2, :, :], in0=src[:, :, :, 0 : N // 2], in1=src[:, :, :, N // 2 : N], op=ALU.add
            )

        def upper_levels(pair):
            cols = slice(2 * pair * TGT, 2 * (pair + 1) * TGT)
            cur = halves[pair][:].rearrange("p f c i j -> p (f c i) j")
            for width in (8, 4, 2):
                nxt = tree.tile([P, 4 * TGT, width], F32, name="lvl%d" % width, tag="lvl%d" % width)
                nc.gpsimd.tensor_tensor(out=nxt[:], in0=cur[:, :, 0:width], in1=cur[:, :, width : 2 * width], op=ALU.add)
                cur = nxt[:]
            last = cur.rearrange("p (f i) j -> p f i j", f=2)
            nc.gpsimd.tensor_tensor(out=s12[:, :, cols], in0=last[:, :, :, 0], in1=last[:, :, :, 1], op=ALU.add)

        def target_term():
            tg = tpsum.tile([P, 2, F], F32, name="tg", tag="tp")
            for hb in range(2):
                for g in range(2):
                    nc.tensor.matmul_mx(
                        out=tg[:, hb, :],
                        lhsT=x_q[:, g, hb * P : (hb + 1) * P].bitcast(FP8X4),
                        lhsT_scale=x_s[:, g, hb * P : (hb + 1) * P],
                        rhs=w_q[:, g, :].bitcast(FP8X4),
                        rhs_scale=w_s[:, g, :],
                        start=(g == 0),
                        stop=(g == 1),
                    )
            nc.scalar.copy(out=c_raw[:], in_=tg[:])

        def target_bias():
            nc.gpsimd.tensor_tensor(
                out=c_sb[:], in0=c_raw[:], in1=bias_bc[:].unsqueeze(1).to_broadcast([P, 2, F]), op=ALU.add
            )

        def finish_tiles(hb):
            fin[hb] = {
                "mean": fpool.tile([P, 2, P], F32, name="mean", tag="mean"),
                "var": fpool.tile([P, 2, P], F32, name="var", tag="var"),
                "msq": fpool.tile([P, P], F32, name="msq", tag="msq"),
            }

        def means_of_summed(hb, width):
            cols = slice(hb * P, hb * P + width)
            nc.scalar.copy(out=fin[hb]["mean"][:, 0, 0:width], in_=bst[:, 0, cols, 1])
            nc.scalar.mul(out=fin[hb]["mean"][:, 1, 0:width], in_=s12[:, 0, cols], mul=1.0 / N)
            nc.scalar.activation(out=fin[hb]["msq"][:, 0:width], in_=s12[:, 0, cols], func=ACT.Square, scale=1.0 / N)

        def variances_of_summed(hb, width):
            cols = slice(hb * P, hb * P + width)
            nc.vector.tensor_scalar_mul(out=fin[hb]["var"][:, 0, 0:width], in0=bst[:, 0, cols, 2], scalar1=1.0 / N)
            nc.vector.scalar_tensor_tensor(
                out=fin[hb]["var"][:, 1, 0:width],
                in0=s12[:, 1, cols],
                scalar=1.0 / N,
                in1=fin[hb]["msq"][:, 0:width],
                op0=ALU.mult,
                op1=ALU.subtract,
            )

        def variances_of_rest(hb, width):
            if width < P:
                cols = slice(hb * P + width, (hb + 1) * P)
                nc.vector.tensor_scalar_mul(out=fin[hb]["var"][:, :, width:P], in0=bst[:, :, cols, 2], scalar1=1.0 / N)
            nc.vector.tensor_scalar_max(out=fin[hb]["var"][:], in0=fin[hb]["var"][:], scalar1=0.0)

        def means_of_rest(hb, width):
            cols = slice(hb * P + width, (hb + 1) * P)
            nc.vector.tensor_copy(out=fin[hb]["mean"][:, :, width:P], in_=bst[:, :, cols, 1])

        def finish_transposes(hb):
            cols = slice(hb * P, (hb + 1) * P)
            fv = tpsum.tile([P, 2, P], F32, name="fv", tag="tp")
            fx = tpsum.tile([P, 2, P], F32, name="fx", tag="tp")
            fm = tpsum.tile([P, 4, P], F32, name="fm", tag="tp")
            for ft in range(2):
                nc.tensor.transpose(fv[:, ft, :], fin[hb]["var"][:, ft, :], ident[:])
            for ft in range(2):
                nc.tensor.transpose(fx[:, ft, :], maxs[:, ft, cols], ident[:])
            for ft in range(2):
                nc.tensor.transpose(fm[:, ft, :], fin[hb]["mean"][:, ft, :], ident[:])
            for ft in range(2):
                nc.tensor.transpose(fm[:, 2 + ft, :], mins[:, ft, cols], ident[:])
            fin[hb]["fv"] = fv
            fin[hb]["fx"] = fx
            fin[hb]["fm"] = fm

        def finish_stores(hb):
            rows = slice(hb * P, (hb + 1) * P)
            hi = fpool.tile([P, 2, F], F32, name="hi", tag="hi")
            lo = fpool.tile([P, 2, F], F32, name="lo", tag="lo")
            nc.scalar.activation(
                out=hi[:, 1, :], in_=fin[hb]["fv"][:].rearrange("p f r -> p (f r)"), func=ACT.Sqrt, bias=eps_t[:]
            )
            nc.vector.tensor_tensor(
                out=hi[:, 0, :], in0=fin[hb]["fx"][:].rearrange("p f r -> p (f r)"), in1=c_sb[:, hb, :], op=ALU.add
            )
            nc.sync.dma_start(out=out_rows[rows, 2 * F : 4 * F], in_=hi[:].rearrange("p s f -> p (s f)"))
            nc.vector.tensor_tensor(
                out=lo[:],
                in0=fin[hb]["fm"][:].rearrange("p (s f) r -> p s (f r)", f=2),
                in1=c_sb[:, hb, :].unsqueeze(1).to_broadcast([P, 2, F]),
                op=ALU.add,
            )
            nc.sync.dma_start(out=out_rows[rows, 0 : 2 * F], in_=lo[:].rearrange("p s f -> p (s f)"))

        def repeat_sources(b0, b1):
            for g in range(2):
                nc.vector.tensor_copy(
                    out=xr_q[:, b0:b1, g, :].bitcast(I32).rearrange("p b (d j) -> p b d j", d=4),
                    in_=x_q[:, g, b0 * N : b1 * N].bitcast(I32).rearrange("p (b j) -> p b j", j=N).unsqueeze(2).to_broadcast([P, b1 - b0, 4, N]),
                )
                nc.vector.tensor_copy(
                    out=xr_s[:, b0:b1, g, :].bitcast(I32).rearrange("p b (d j) -> p b d j", d=4),
                    in_=x_s[:, g, b0 * N : b1 * N].bitcast(I32).rearrange("p (b j) -> p b j", j=N // 4).unsqueeze(2).to_broadcast([P, b1 - b0, 4, N // 4]),
                )

        nc.sync.dma_start(out=x_raw[:], in_=x.flatten_outer_dims().rearrange("(t p) k -> p t k", p=P))
        load(0, 4)
        load_w(2)
        load_w(1)
        load(1)
        load(2)
        load_w(0)
        nc.sync.dma_start(out=bias_bc[:], in_=b_pre.partition_broadcast(P))
        load(3)
        load(4)

        nc.vector.memset(eps_t[:], EPS_STD)
        nc.vector.memset(warm[:], 1.0)
        nc.vector.memset(x_s[:].rearrange("p g n -> p (g n)").bitcast(I32), 0)
        nc.scalar.sqrt(warm[:], warm[:])
        make_identity(nc, ident[:])
        regroup_w_gpsimd(0)

        for t in range(2):
            tp = transpose_rows(x_raw[:, t, :])
            evacuate(tp, x_grp[:, :, t * P : (t + 1) * P, :])
        quantise(
            x_grp[:].rearrange("p g n u -> p (g n u)").bitcast(BF16),
            x_q[:].rearrange("p g n -> p (g n)"),
            x_s[:].rearrange("p g n -> p (g n)"),
        )
        repeat_sources(0, 1)
        regroup_w_vector(2)
        quantise_w(2)

        LAST = P - 2 * TGT
        for n in range(-2, NCH + 1):
            if 0 <= n and n + PRELOAD < NCH:
                load(n + PRELOAD)
            if n == 11:
                finish_tiles(0)
                means_of_summed(0, P)
            if n + 2 < NCH:
                front(n + 2)
            if n == 13:
                finish_transposes(0)
            if 0 <= n < NCH:
                messages(n)
            if n == 4:
                target_term()
            if n == 12:
                variances_of_summed(0, P)
                variances_of_rest(0, P)
            if n == 14:
                finish_stores(0)
            if n == 3:
                quantise_w(0)
            if 0 <= n + 1 < NCH:
                quantise_chunk(n + 1)
            if n == -1:
                regroup_w_vector(1)
                quantise_w(1)
                repeat_sources(1, B)
            if n == 16:
                finish_tiles(1)
                means_of_summed(1, LAST)
                variances_of_summed(1, LAST)
            if n >= 1:
                reduces(n - 1)
                if n - 1 < SUMMED:
                    first_level(n - 1)
                    if (n - 1) % 2 == 1:
                        upper_levels((n - 1) // 2)
            if n == 6:
                target_bias()
        variances_of_rest(1, LAST)
        means_of_rest(1, LAST)
        finish_transposes(1)
        finish_stores(1)
